import numpy as np
import ml_dtypes


def mxq(x, axis, fmt="e4m3"):
    dtype, down = {"e4m3": (ml_dtypes.float8_e4m3fn, 7), "e5m2": (ml_dtypes.float8_e5m2, 14)}[fmt]
    v = np.moveaxis(np.asarray(x, np.float32).astype(ml_dtypes.bfloat16).astype(np.float64), axis, -1)
    blocks = v.reshape(v.shape[:-1] + (-1, 32))
    amax = np.abs(blocks).max(-1, keepdims=True)
    byte = np.maximum(np.where(amax > 0, np.frexp(amax)[1] - 1 + 127, 0) - down, 1)
    scale = np.exp2(byte - 127.0)
    codes = (blocks / scale).astype(np.float32).astype(dtype).astype(np.float64)
    return np.moveaxis((codes * scale).reshape(v.shape), -1, axis)


WIDE = False


def mx_kscale(k):
    if not WIDE:
        return np.ones(k)
    levels = np.array([10, -10, 5, -5, 0])
    a = np.random.permutation(np.resize(levels, k // 512 * 4)).reshape(k // 512, 4)
    idx = np.arange(k)
    return np.exp2(a[idx // 512, idx % 128 // 32])


BF16 = ml_dtypes.bfloat16


def bf(x):
    return np.asarray(x, np.float32).astype(BF16)


def f64(x):
    return np.asarray(x).astype(np.float64)


E2M1 = np.array([0.0, 0.5, 1.0, 1.5, 2.0, 3.0, 4.0, 6.0, -0.0, -0.5, -1.0, -1.5, -2.0, -3.0, -4.0, -6.0])


def pack_weight(w, fmt):
    k, n = w.shape
    w = f64(bf(w)).reshape(k // 32, 32, n)
    amax = np.abs(w).max(1)
    if fmt == "e4m3":
        byte = np.frexp(amax)[1] - 1 + 127 - 7
    else:
        mant, ex = np.frexp(amax / 6.0)
        byte = np.where(mant > 0.5, ex, ex - 1) + 127
    byte = np.clip(np.where(amax > 0, byte, 1), 1, 254)
    scaled = (w * np.exp2(127.0 - byte)[:, None, :]).reshape(k, n).astype(np.float32)
    by_word = np.ascontiguousarray(scaled.reshape(k // 512, 128, 4, n).transpose(0, 1, 3, 2))
    if fmt == "e4m3":
        words = by_word.astype(ml_dtypes.float8_e4m3fn).view(np.uint8)
    else:
        c = by_word.astype(ml_dtypes.float4_e2m1fn).view(np.uint8) & 0xF
        words = c[..., 0::2] | (c[..., 1::2] << 4)
    return np.ascontiguousarray(words), np.ascontiguousarray(byte.astype(np.uint8).reshape(k // 512, 16, n))


def unpack_weight(words, scales, fmt):
    g, p, n, _ = words.shape
    if fmt == "e4m3":
        vals = np.ascontiguousarray(words).view(ml_dtypes.float8_e4m3fn).astype(np.float64)
    else:
        nib = np.empty((g, p, n, 4), np.uint8)
        nib[..., 0::2] = words & 0xF
        nib[..., 1::2] = words >> 4
        vals = E2M1[nib]
    vals = vals * np.repeat(np.exp2(scales.astype(np.float64) - 127.0), 8, axis=1)[..., None]
    return vals.transpose(0, 1, 3, 2).reshape(g * 512, n)


B, IN, OUT = 512, 2048, 1536

EPS = 1e-07


def sigmoid(v):
    return 1.0 / (1.0 + np.exp(-v))


def setup_inputs():
    s = mx_kscale(IN)
    u = s / s.min()
    input_tensor = bf(np.random.standard_normal((B, IN)) * u)
    W_hat = bf(np.random.standard_normal((IN, OUT)) * 1.0 / np.sqrt(IN) / u[:, None])
    M_hat = bf(np.random.standard_normal((IN, OUT)) * 1.0)
    gate_words, gate_scales = pack_weight(np.random.standard_normal((IN, OUT)) * 1.0 / np.sqrt(IN) / u[:, None], "e4m3")
    return {"input_tensor": input_tensor,
            "W_hat": W_hat,
            "M_hat": M_hat,
            "gate_words": gate_words,
            "gate_scales": gate_scales}


def reference(input_tensor, W_hat, M_hat, gate_words, gate_scales):
    x = f64(input_tensor)
    W = np.tanh(f64(W_hat)) * sigmoid(f64(M_hat))
    xq = mxq(x, 1, "e4m3")
    Wq = mxq(W, 0, "e4m3")
    a = xq @ Wq
    m = np.exp(mxq(np.log(np.abs(x) + EPS), 1, "e4m3") @ Wq)
    g = sigmoid(xq @ unpack_weight(gate_words, gate_scales, "e4m3"))
    return g * a + (1.0 - g) * m

@@ -1,0 +1,269 @@
+from contextlib import ExitStack
+
+import concourse.mybir as mybir
+from concourse.masks import make_identity
+
+BF16 = mybir.dt.bfloat16
+F32 = mybir.dt.float32
+I32 = mybir.dt.int32
+U32 = mybir.dt.uint32
+U8 = mybir.dt.uint8
+FP8X4 = mybir.dt.float8_e4m3fn_x4
+ACT = mybir.ActivationFunctionType
+ALU = mybir.AluOpType
+
+B, IN, OUT = 512, 2048, 1536
+EPS = 1e-07
+FLOPS = 3 * 2 * B * IN * OUT
+
+P = 128
+PACK = 4
+K_PASS = P * PACK
+PASSES = IN // K_PASS
+ROW_TILES = B // P
+PAIRS = ROW_TILES // 2
+CHUNK = 256
+CHUNKS = OUT // CHUNK
+SLAB = 2 * CHUNK
+SLABS = OUT // SLAB
+X_UNITS = 2 * ROW_TILES
+UNIT_K = 2 * K_PASS
+ABS_MASK = 0x7FFF7FFF
+
+
+def tile_nalu_kernel(tc, input_tensor, W_hat, M_hat, gate_words, gate_scales, out):
+    nc = tc.nc
+    with ExitStack() as stack:
+        keep = stack.enter_context(tc.tile_pool(name="keep", bufs=1))
+        x_pool = stack.enter_context(tc.tile_pool(name="x_pool", bufs=X_UNITS))
+        slabs = stack.enter_context(tc.tile_pool(name="slabs", bufs=2))
+        stream = stack.enter_context(tc.tile_pool(name="stream", bufs=3))
+        blend = stack.enter_context(tc.tile_pool(name="blend", bufs=2))
+        psum = stack.enter_context(tc.psum_pool(name="psum", bufs=2))
+        stack.enter_context(tc.manual_schedule())
+
+        identity = keep.tile([P, P], F32, name="identity")
+        make_identity(nc, identity[:])
+
+        x_codes = keep.tile([P, ROW_TILES, PASSES, P], U32, name="x_codes", align_bytes=64)
+        x_scales = keep.tile([P, ROW_TILES, PASSES, P], U8, name="x_scales", align_bytes=64)
+        log_codes = keep.tile([P, ROW_TILES, PASSES, P], U32, name="log_codes", align_bytes=64)
+        log_scales = keep.tile([P, ROW_TILES, PASSES, P], U8, name="log_scales", align_bytes=64)
+
+        gate_planes = keep.tile([P, OUT], U8, name="gate_planes", align_bytes=64)
+        nc.vector.memset(gate_planes[:].bitcast(I32), 0)
+
+        x_rows = {}
+
+        def load_x(unit):
+            row_tile, half = divmod(unit, 2)
+            x_rows[unit] = x_pool.tile([P, UNIT_K], BF16, name="x_rows")
+            nc.sync.dma_start(
+                out=x_rows[unit][:],
+                in_=input_tensor[P * row_tile : P * (row_tile + 1), UNIT_K * half : UNIT_K * (half + 1)],
+            )
+
+        def load_gate_planes():
+            for quadrant in range(4):
+                nc.sync.dma_start(
+                    out=gate_planes[32 * quadrant : 32 * quadrant + 16, :].bitcast(I32),
+                    in_=gate_scales[:, 4 * quadrant : 4 * quadrant + 4, :].bitcast(I32),
+                )
+
+        hat_slabs = {}
+
+        def load_slab(slab):
+            cols = slice(SLAB * slab, SLAB * (slab + 1))
+            w_slab = slabs.tile([P, PASSES, PACK, SLAB], BF16, name="w_slab")
+            m_slab = slabs.tile([P, PASSES, PACK, SLAB], BF16, name="m_slab")
+            for g in range(PASSES):
+                k_rows = slice(K_PASS * g, K_PASS * (g + 1))
+                nc.sync.dma_start(
+                    out=w_slab[:, g], in_=W_hat[k_rows, cols].rearrange("(p j) n -> p j n", j=PACK)
+                )
+                nc.sync.dma_start(
+                    out=m_slab[:, g], in_=M_hat[k_rows, cols].rearrange("(p j) n -> p j n", j=PACK)
+                )
+            hat_slabs[slab] = (w_slab, m_slab)
+
+        gate_codes = {}
+
+        def load_gate(chunk):
+            cols = slice(CHUNK * chunk, CHUNK * (chunk + 1))
+            gate_codes[chunk] = stream.tile([P, PASSES, CHUNK], I32, name="gate_codes", align_bytes=64)
+            nc.sync.dma_start(
+                out=gate_codes[chunk][:],
+                in_=gate_words[:, :, cols, :].rearrange("g p n t -> p g (n t)").bitcast(I32),
+            )
+
+        x_grouped = {}
+        log_grouped = {}
+
+        def prepare_x(unit):
+            words = x_rows[unit][:].bitcast(F32)
+            x_t = psum.tile([P, 2, 2, P], F32, name="x_t")
+            for g in range(2):
+                for w in range(2):
+                    nc.tensor.transpose(
+                        x_t[:, g, w, :], words[:, 256 * g + w : 256 * (g + 1) : 2], identity[:]
+                    )
+            x_grouped[unit] = x_pool.tile([P, UNIT_K], BF16, name="x_grouped", align_bytes=64)
+            nc.vector.tensor_copy(
+                out=x_grouped[unit][:].bitcast(F32).rearrange("p (g r w) -> p g r w", g=2, w=2),
+                in_=x_t[:].rearrange("p g w r -> p g r w"),
+            )
+            x_abs = stream.tile([P, UNIT_K], BF16, name="x_abs")
+            nc.vector.tensor_scalar(
+                out=x_abs[:].bitcast(I32),
+                in0=x_grouped[unit][:].bitcast(I32),
+                scalar1=ABS_MASK,
+                scalar2=None,
+                op0=ALU.bitwise_and,
+            )
+            log_grouped[unit] = x_pool.tile([P, UNIT_K], BF16, name="log_grouped", align_bytes=64)
+            nc.scalar.activation(out=log_grouped[unit][:], in_=x_abs[:], func=ACT.Ln, bias=EPS, scale=1.0)
+
+        def quantise_unit(grouped, codes, scales, unit):
+            row_tile, half = divmod(unit, 2)
+            passes = slice(2 * half, 2 * half + 2)
+            nc.vector.quantize_mx(
+                out=codes[:, row_tile, passes, :].rearrange("p g r -> p (g r)").bitcast(FP8X4),
+                scales=scales[:, row_tile, passes, :].rearrange("p g r -> p (g r)"),
+                in_=grouped[unit][:],
+            )
+
+        w_codes = {}
+        w_scales = {}
+        w_grouped = {}
+
+        def make_twice_w(chunk, g):
+            w_slab, m_slab = hat_slabs[chunk // 2]
+            cols = slice(CHUNK * (chunk % 2), CHUNK * (chunk % 2 + 1))
+            tanh_w = stream.tile([P, PACK, CHUNK], F32, name="tanh_w")
+            tanh_m = stream.tile([P, PACK, CHUNK], F32, name="tanh_m")
+            nc.scalar.activation(out=tanh_w[:], in_=w_slab[:, g, :, cols], func=ACT.Tanh)
+            nc.scalar.activation(out=tanh_m[:], in_=m_slab[:, g, :, cols], func=ACT.Tanh, scale=0.5)
+            w_grouped[g] = stream.tile([P, CHUNK, PACK], BF16, name="w_grouped", align_bytes=64)
+            nc.vector.scalar_tensor_tensor(
+                out=w_grouped[g][:],
+                in0=tanh_m[:].rearrange("p j n -> p n j"),
+                scalar=1.0,
+                in1=tanh_w[:].rearrange("p j n -> p n j"),
+                op0=ALU.add,
+                op1=ALU.mult,
+            )
+
+        def quantise_w(chunk, g):
+            if g == 0:
+                w_codes[chunk] = blend.tile([P, PASSES, CHUNK], U32, name="w_codes", align_bytes=64)
+                w_scales[chunk] = blend.tile([P, PASSES, CHUNK], U8, name="w_scales", align_bytes=64)
+            nc.vector.quantize_mx(
+                out=w_codes[chunk][:, g, :].bitcast(FP8X4),
+                scales=w_scales[chunk][:, g, :],
+                in_=w_grouped[g][:].rearrange("p n j -> p (n j)"),
+            )
+
+        def multiply(bank, pair, lhs_codes, lhs_scales, rhs_codes, rhs_scale_of_pass):
+            for i in range(2):
+                row_tile = 2 * pair + i
+                for g in range(PASSES):
+                    nc.tensor.matmul_mx(
+                        out=bank[:, i, :],
+                        lhsT=lhs_codes[:, row_tile, g, :].bitcast(FP8X4),
+                        lhsT_scale=lhs_scales[:, row_tile, g, :],
+                        rhs=rhs_codes[:, g, :].bitcast(FP8X4),
+                        rhs_scale=rhs_scale_of_pass(g),
+                        start=(g == 0),
+                        stop=(g == PASSES - 1),
+                    )
+
+        gate_sums = {}
+        log_sums = {}
+        add_sums = {}
+        gate_tanh = {}
+
+        def multiply_gate(chunk):
+            cols = slice(CHUNK * chunk, CHUNK * (chunk + 1))
+            for pair in range(PAIRS):
+                gate_sums[pair] = psum.tile([P, 2, CHUNK], F32, name="gate_sums")
+                multiply(
+                    gate_sums[pair], pair, x_codes, x_scales, gate_codes[chunk],
+                    lambda g: gate_planes[4 * g : P, cols],
+                )
+
+        def multiply_w(chunk):
+            for pair in range(PAIRS):
+                log_sums[pair] = psum.tile([P, 2, CHUNK], F32, name="log_sums")
+                multiply(
+                    log_sums[pair], pair, log_codes, log_scales, w_codes[chunk],
+                    lambda g: w_scales[chunk][:, g, :],
+                )
+                add_sums[pair] = psum.tile([P, 2, CHUNK], F32, name="add_sums")
+                multiply(
+                    add_sums[pair], pair, x_codes, x_scales, w_codes[chunk],
+                    lambda g: w_scales[chunk][:, g, :],
+                )
+
+        def squash_gate(pair):
+            gate_tanh[pair] = blend.tile([P, 2, CHUNK], F32, name="gate_tanh")
+            nc.scalar.activation(out=gate_tanh[pair][:], in_=gate_sums[pair][:], func=ACT.Tanh, scale=0.5)
+
+        def blend_and_store(chunk, pair):
+            mult_path = blend.tile([P, 2, CHUNK], F32, name="mult_path")
+            nc.scalar.activation(out=mult_path[:], in_=log_sums[pair][:], func=ACT.Exp, scale=0.5)
+            diff = blend.tile([P, 2, CHUNK], F32, name="diff")
+            nc.vector.scalar_tensor_tensor(
+                out=diff[:], in0=add_sums[pair][:], scalar=0.5, in1=mult_path[:],
+                op0=ALU.mult, op1=ALU.subtract,
+            )
+            gated = blend.tile([P, 2, CHUNK], F32, name="gated")
+            nc.vector.scalar_tensor_tensor(
+                out=gated[:], in0=gate_tanh[pair][:], scalar=1.0, in1=diff[:],
+                op0=ALU.add, op1=ALU.mult,
+            )
+            result = blend.tile([P, 2, CHUNK], F32, name="result")
+            nc.vector.scalar_tensor_tensor(
+                out=result[:], in0=gated[:], scalar=0.5, in1=mult_path[:],
+                op0=ALU.mult, op1=ALU.add,
+            )
+            nc.sync.dma_start(
+                out=out[2 * P * pair : 2 * P * (pair + 1), CHUNK * chunk : CHUNK * (chunk + 1)].rearrange(
+                    "(i p) n -> p i n", p=P
+                ),
+                in_=result[:],
+            )
+
+        for unit in range(X_UNITS):
+            load_x(unit)
+        load_gate_planes()
+        load_slab(0)
+        load_gate(0)
+        load_gate(1)
+        load_slab(1)
+        load_gate(2)
+
+        for unit in range(X_UNITS):
+            prepare_x(unit)
+        for unit in range(X_UNITS):
+            quantise_unit(x_grouped, x_codes, x_scales, unit)
+        for unit in range(X_UNITS):
+            quantise_unit(log_grouped, log_codes, log_scales, unit)
+        multiply_gate(0)
+
+        for chunk in range(CHUNKS):
+            for g in range(PASSES):
+                make_twice_w(chunk, g)
+                if chunk > 0 and g in (1, 2):
+                    blend_and_store(chunk - 1, g - 1)
+                quantise_w(chunk, g)
+            for pair in range(PAIRS):
+                squash_gate(pair)
+            multiply_w(chunk)
+            if chunk + 1 < CHUNKS:
+                multiply_gate(chunk + 1)
+            if chunk + 3 < CHUNKS:
+                load_gate(chunk + 3)
+            if chunk % 2 == 1 and chunk // 2 + 2 < SLABS:
+                load_slab(chunk // 2 + 2)
+        for pair in range(PAIRS):
+            blend_and_store(CHUNKS - 1, pair)

@@ -139,16 +139,25 @@ def tile_nalu_kernel(tc, input_tensor, W_hat, M_hat, gate_words, gate_scales, ou
         def make_twice_w(chunk, g):
             w_slab, m_slab = hat_slabs[chunk // 2]
             cols = slice(CHUNK * (chunk % 2), CHUNK * (chunk % 2 + 1))
-            tanh_w = stream.tile([P, PACK, CHUNK], F32, name="tanh_w")
-            tanh_m = stream.tile([P, PACK, CHUNK], F32, name="tanh_m")
-            nc.scalar.activation(out=tanh_w[:], in_=w_slab[:, g, :, cols], func=ACT.Tanh)
-            nc.scalar.activation(out=tanh_m[:], in_=m_slab[:, g, :, cols], func=ACT.Tanh, scale=0.5)
+            tanh_w = stream.tile([P, 2, CHUNK, 2], F32, name="tanh_w")
+            tanh_m = stream.tile([P, 2, CHUNK, 2], F32, name="tanh_m")
+            nc.scalar.activation(
+                out=tanh_w[:],
+                in_=w_slab[:, g, :, cols].rearrange("p (a b) n -> p b n a", b=2),
+                func=ACT.Tanh,
+            )
+            nc.scalar.activation(
+                out=tanh_m[:],
+                in_=m_slab[:, g, :, cols].rearrange("p (a b) n -> p b n a", b=2),
+                func=ACT.Tanh,
+                scale=0.5,
+            )
             w_grouped[g] = stream.tile([P, CHUNK, PACK], BF16, name="w_grouped", align_bytes=64)
             nc.vector.scalar_tensor_tensor(
-                out=w_grouped[g][:],
-                in0=tanh_m[:].rearrange("p j n -> p n j"),
+                out=w_grouped[g][:].rearrange("p n (a b) -> p (n a) b", b=2),
+                in0=tanh_m[:].rearrange("p b n a -> p (n a) b"),
                 scalar=1.0,
-                in1=tanh_w[:].rearrange("p j n -> p n j"),
+                in1=tanh_w[:].rearrange("p b n a -> p (n a) b"),
                 op0=ALU.add,
                 op1=ALU.mult,
             )

@@ -23,11 +23,14 @@ PASSES = IN // K_PASS
 ROW_TILES = B // P
 PAIRS = ROW_TILES // 2
 CHUNK = 256
-CHUNKS = OUT // CHUNK
+CHUNK_WIDTHS = [CHUNK] * (OUT // CHUNK - 1) + [CHUNK // 2] * 2
+CHUNK_STARTS = [sum(CHUNK_WIDTHS[:c]) for c in range(len(CHUNK_WIDTHS))]
+CHUNKS = len(CHUNK_WIDTHS)
 SLAB = 2 * CHUNK
 SLABS = OUT // SLAB
 X_UNITS = 2 * ROW_TILES
 UNIT_K = 2 * K_PASS
+EARLY_BANKS = "x_t_then_gate_sums"
 ABS_MASK = 0x7FFF7FFF
 
 
@@ -86,22 +89,29 @@ def tile_nalu_kernel(tc, input_tensor, W_hat, M_hat, gate_words, gate_scales, ou
                 )
             hat_slabs[slab] = (w_slab, m_slab)
 
-        gate_codes = {}
+        gate_slabs = {}
 
-        def load_gate(chunk):
-            cols = slice(CHUNK * chunk, CHUNK * (chunk + 1))
-            gate_codes[chunk] = stream.tile([P, PASSES, CHUNK], I32, name="gate_codes", align_bytes=64)
+        def load_gate_slab(slab):
+            cols = slice(SLAB * slab, SLAB * (slab + 1))
+            gate_slabs[slab] = slabs.tile([P, PASSES, SLAB], I32, name="gate_slab", align_bytes=64)
             nc.sync.dma_start(
-                out=gate_codes[chunk][:],
+                out=gate_slabs[slab][:],
                 in_=gate_words[:, :, cols, :].rearrange("g p n t -> p g (n t)").bitcast(I32),
             )
+
+        def columns_in_slab(chunk):
+            first = CHUNK_STARTS[chunk] % SLAB
+            return CHUNK_STARTS[chunk] // SLAB, slice(first, first + CHUNK_WIDTHS[chunk])
+
+        def columns(chunk):
+            return slice(CHUNK_STARTS[chunk], CHUNK_STARTS[chunk] + CHUNK_WIDTHS[chunk])
 
         x_grouped = {}
         log_grouped = {}
 
         def prepare_x(unit):
             words = x_rows[unit][:].bitcast(F32)
-            x_t = psum.tile([P, 2, 2, P], F32, name="x_t")
+            x_t = psum.tile([P, 2, 2, P], F32, name="x_t", tag=EARLY_BANKS, bufs=4)
             for g in range(2):
                 for w in range(2):
                     nc.tensor.transpose(
@@ -137,10 +147,11 @@ def tile_nalu_kernel(tc, input_tensor, W_hat, M_hat, gate_words, gate_scales, ou
         w_grouped = {}
 
         def make_twice_w(chunk, g):
-            w_slab, m_slab = hat_slabs[chunk // 2]
-            cols = slice(CHUNK * (chunk % 2), CHUNK * (chunk % 2 + 1))
-            tanh_w = stream.tile([P, 2, CHUNK, 2], F32, name="tanh_w")
-            tanh_m = stream.tile([P, 2, CHUNK, 2], F32, name="tanh_m")
+            slab, cols = columns_in_slab(chunk)
+            w_slab, m_slab = hat_slabs[slab]
+            width = CHUNK_WIDTHS[chunk]
+            tanh_w = stream.tile([P, 2, width, 2], F32, name="tanh_w")
+            tanh_m = stream.tile([P, 2, width, 2], F32, name="tanh_m")
             nc.scalar.activation(
                 out=tanh_w[:],
                 in_=w_slab[:, g, :, cols].rearrange("p (a b) n -> p b n a", b=2),
@@ -152,7 +163,7 @@ def tile_nalu_kernel(tc, input_tensor, W_hat, M_hat, gate_words, gate_scales, ou
                 func=ACT.Tanh,
                 scale=0.5,
             )
-            w_grouped[g] = stream.tile([P, CHUNK, PACK], BF16, name="w_grouped", align_bytes=64)
+            w_grouped[g] = stream.tile([P, width, PACK], BF16, name="w_grouped", align_bytes=64)
             nc.vector.scalar_tensor_tensor(
                 out=w_grouped[g][:].rearrange("p n (a b) -> p (n a) b", b=2),
                 in0=tanh_m[:].rearrange("p b n a -> p (n a) b"),
@@ -164,15 +175,16 @@ def tile_nalu_kernel(tc, input_tensor, W_hat, M_hat, gate_words, gate_scales, ou
 
         def quantise_w(chunk, g):
             if g == 0:
-                w_codes[chunk] = blend.tile([P, PASSES, CHUNK], U32, name="w_codes", align_bytes=64)
-                w_scales[chunk] = blend.tile([P, PASSES, CHUNK], U8, name="w_scales", align_bytes=64)
+                width = CHUNK_WIDTHS[chunk]
+                w_codes[chunk] = blend.tile([P, PASSES, width], U32, name="w_codes", align_bytes=64)
+                w_scales[chunk] = blend.tile([P, PASSES, width], U8, name="w_scales", align_bytes=64)
             nc.vector.quantize_mx(
                 out=w_codes[chunk][:, g, :].bitcast(FP8X4),
                 scales=w_scales[chunk][:, g, :],
                 in_=w_grouped[g][:].rearrange("p n j -> p (n j)"),
             )
 
-        def multiply(bank, pair, lhs_codes, lhs_scales, rhs_codes, rhs_scale_of_pass):
+        def multiply(bank, pair, lhs_codes, lhs_scales, rhs_of_pass, rhs_scale_of_pass):
             for i in range(2):
                 row_tile = 2 * pair + i
                 for g in range(PASSES):
@@ -180,7 +192,7 @@ def tile_nalu_kernel(tc, input_tensor, W_hat, M_hat, gate_words, gate_scales, ou
                         out=bank[:, i, :],
                         lhsT=lhs_codes[:, row_tile, g, :].bitcast(FP8X4),
                         lhsT_scale=lhs_scales[:, row_tile, g, :],
-                        rhs=rhs_codes[:, g, :].bitcast(FP8X4),
+                        rhs=rhs_of_pass(g).bitcast(FP8X4),
                         rhs_scale=rhs_scale_of_pass(g),
                         start=(g == 0),
                         stop=(g == PASSES - 1),
@@ -192,53 +204,65 @@ def tile_nalu_kernel(tc, input_tensor, W_hat, M_hat, gate_words, gate_scales, ou
         gate_tanh = {}
 
         def multiply_gate(chunk):
-            cols = slice(CHUNK * chunk, CHUNK * (chunk + 1))
+            slab, cols = columns_in_slab(chunk)
             for pair in range(PAIRS):
-                gate_sums[pair] = psum.tile([P, 2, CHUNK], F32, name="gate_sums")
+                gate_sums[chunk, pair] = psum.tile(
+                    [P, 2, CHUNK_WIDTHS[chunk]], F32, name="gate_sums", tag=EARLY_BANKS, bufs=4
+                )
                 multiply(
-                    gate_sums[pair], pair, x_codes, x_scales, gate_codes[chunk],
-                    lambda g: gate_planes[4 * g : P, cols],
+                    gate_sums[chunk, pair], pair, x_codes, x_scales,
+                    lambda g: gate_slabs[slab][:, g, cols],
+                    lambda g: gate_planes[4 * g : P, columns(chunk)],
                 )
 
         def multiply_w(chunk):
             for pair in range(PAIRS):
-                log_sums[pair] = psum.tile([P, 2, CHUNK], F32, name="log_sums")
+                log_sums[pair] = psum.tile([P, 2, CHUNK_WIDTHS[chunk]], F32, name="log_sums")
                 multiply(
-                    log_sums[pair], pair, log_codes, log_scales, w_codes[chunk],
+                    log_sums[pair], pair, log_codes, log_scales,
+                    lambda g: w_codes[chunk][:, g, :],
                     lambda g: w_scales[chunk][:, g, :],
                 )
-                add_sums[pair] = psum.tile([P, 2, CHUNK], F32, name="add_sums")
+                add_sums[pair] = psum.tile([P, 2, CHUNK_WIDTHS[chunk]], F32, name="add_sums")
                 multiply(
-                    add_sums[pair], pair, x_codes, x_scales, w_codes[chunk],
+                    add_sums[pair], pair, x_codes, x_scales,
+                    lambda g: w_codes[chunk][:, g, :],
                     lambda g: w_scales[chunk][:, g, :],
                 )
 
-        def squash_gate(pair):
-            gate_tanh[pair] = blend.tile([P, 2, CHUNK], F32, name="gate_tanh")
-            nc.scalar.activation(out=gate_tanh[pair][:], in_=gate_sums[pair][:], func=ACT.Tanh, scale=0.5)
+        mult_path = {}
+        diff = {}
 
-        def blend_and_store(chunk, pair):
-            mult_path = blend.tile([P, 2, CHUNK], F32, name="mult_path")
-            nc.scalar.activation(out=mult_path[:], in_=log_sums[pair][:], func=ACT.Exp, scale=0.5)
-            diff = blend.tile([P, 2, CHUNK], F32, name="diff")
+        def squash_gate(chunk, pair):
+            gate_tanh[chunk, pair] = stream.tile([P, 2, CHUNK_WIDTHS[chunk]], F32, name="gate_tanh")
+            nc.scalar.activation(
+                out=gate_tanh[chunk, pair][:], in_=gate_sums[chunk, pair][:], func=ACT.Tanh, scale=0.5
+            )
+
+        def start_blend(chunk, pair):
+            shape = [P, 2, CHUNK_WIDTHS[chunk]]
+            mult_path[pair] = blend.tile(shape, F32, name="mult_path")
+            nc.scalar.activation(out=mult_path[pair][:], in_=log_sums[pair][:], func=ACT.Exp, scale=0.5)
+            diff[pair] = blend.tile(shape, F32, name="diff")
             nc.vector.scalar_tensor_tensor(
-                out=diff[:], in0=add_sums[pair][:], scalar=0.5, in1=mult_path[:],
+                out=diff[pair][:], in0=add_sums[pair][:], scalar=0.5, in1=mult_path[pair][:],
                 op0=ALU.mult, op1=ALU.subtract,
             )
-            gated = blend.tile([P, 2, CHUNK], F32, name="gated")
+
+        def finish_blend(chunk, pair):
+            shape = [P, 2, CHUNK_WIDTHS[chunk]]
+            gated = blend.tile(shape, F32, name="gated")
             nc.vector.scalar_tensor_tensor(
-                out=gated[:], in0=gate_tanh[pair][:], scalar=1.0, in1=diff[:],
+                out=gated[:], in0=gate_tanh[chunk, pair][:], scalar=1.0, in1=diff[pair][:],
                 op0=ALU.add, op1=ALU.mult,
             )
-            result = blend.tile([P, 2, CHUNK], F32, name="result")
+            result = blend.tile(shape, F32, name="result")
             nc.vector.scalar_tensor_tensor(
-                out=result[:], in0=gated[:], scalar=0.5, in1=mult_path[:],
+                out=result[:], in0=gated[:], scalar=0.5, in1=mult_path[pair][:],
                 op0=ALU.mult, op1=ALU.add,
             )
             nc.sync.dma_start(
-                out=out[2 * P * pair : 2 * P * (pair + 1), CHUNK * chunk : CHUNK * (chunk + 1)].rearrange(
-                    "(i p) n -> p i n", p=P
-                ),
+                out=out[2 * P * pair : 2 * P * (pair + 1), columns(chunk)].rearrange("(i p) n -> p i n", p=P),
                 in_=result[:],
             )
 
@@ -246,10 +270,9 @@ def tile_nalu_kernel(tc, input_tensor, W_hat, M_hat, gate_words, gate_scales, ou
             load_x(unit)
         load_gate_planes()
         load_slab(0)
-        load_gate(0)
-        load_gate(1)
+        load_gate_slab(0)
         load_slab(1)
-        load_gate(2)
+        load_gate_slab(1)
 
         for unit in range(X_UNITS):
             prepare_x(unit)
@@ -258,21 +281,28 @@ def tile_nalu_kernel(tc, input_tensor, W_hat, M_hat, gate_words, gate_scales, ou
         for unit in range(X_UNITS):
             quantise_unit(log_grouped, log_codes, log_scales, unit)
         multiply_gate(0)
+        multiply_gate(1)
 
         for chunk in range(CHUNKS):
             for g in range(PASSES):
+                pair = g - (PASSES - PAIRS)
+                weave = chunk > 0 and pair >= 0
                 make_twice_w(chunk, g)
-                if chunk > 0 and g in (1, 2):
-                    blend_and_store(chunk - 1, g - 1)
+                if weave:
+                    start_blend(chunk - 1, pair)
                 quantise_w(chunk, g)
+                if weave:
+                    finish_blend(chunk - 1, pair)
             for pair in range(PAIRS):
-                squash_gate(pair)
+                squash_gate(chunk, pair)
             multiply_w(chunk)
-            if chunk + 1 < CHUNKS:
-                multiply_gate(chunk + 1)
-            if chunk + 3 < CHUNKS:
-                load_gate(chunk + 3)
-            if chunk % 2 == 1 and chunk // 2 + 2 < SLABS:
-                load_slab(chunk // 2 + 2)
+            if chunk + 2 < CHUNKS:
+                multiply_gate(chunk + 2)
+            chunk_end = CHUNK_STARTS[chunk] + CHUNK_WIDTHS[chunk]
+            next_slab = chunk_end // SLAB + 1
+            if chunk_end % SLAB == 0 and next_slab < SLABS:
+                load_slab(next_slab)
+                load_gate_slab(next_slab)
         for pair in range(PAIRS):
-            blend_and_store(CHUNKS - 1, pair)
+            start_blend(CHUNKS - 1, pair)
+            finish_blend(CHUNKS - 1, pair)

@@ -232,33 +232,38 @@ def tile_nalu_kernel(tc, input_tensor, W_hat, M_hat, gate_words, gate_scales, ou
 
         mult_path = {}
         diff = {}
+        gated = {}
 
         def squash_gate(chunk, pair):
-            gate_tanh[chunk, pair] = stream.tile([P, 2, CHUNK_WIDTHS[chunk]], F32, name="gate_tanh")
+            gate_tanh[chunk, pair] = stream.tile([P, 2, CHUNK_WIDTHS[chunk]], F32, name="gate_tanh", bufs=4)
             nc.scalar.activation(
                 out=gate_tanh[chunk, pair][:], in_=gate_sums[chunk, pair][:], func=ACT.Tanh, scale=0.5
             )
 
+        def exponentiate(chunk, pair):
+            mult_path[pair] = blend.tile([P, 2, CHUNK_WIDTHS[chunk]], F32, name="mult_path")
+            nc.scalar.activation(out=mult_path[pair][:], in_=log_sums[pair][:], func=ACT.Exp, scale=0.5)
+
         def start_blend(chunk, pair):
             shape = [P, 2, CHUNK_WIDTHS[chunk]]
-            mult_path[pair] = blend.tile(shape, F32, name="mult_path")
-            nc.scalar.activation(out=mult_path[pair][:], in_=log_sums[pair][:], func=ACT.Exp, scale=0.5)
             diff[pair] = blend.tile(shape, F32, name="diff")
             nc.vector.scalar_tensor_tensor(
                 out=diff[pair][:], in0=add_sums[pair][:], scalar=0.5, in1=mult_path[pair][:],
                 op0=ALU.mult, op1=ALU.subtract,
             )
 
-        def finish_blend(chunk, pair):
-            shape = [P, 2, CHUNK_WIDTHS[chunk]]
-            gated = blend.tile(shape, F32, name="gated")
+        def apply_gate(chunk, pair):
+            gated[pair] = blend.tile([P, 2, CHUNK_WIDTHS[chunk]], F32, name="gated")
             nc.vector.scalar_tensor_tensor(
-                out=gated[:], in0=gate_tanh[chunk, pair][:], scalar=1.0, in1=diff[pair][:],
+                out=gated[pair][:], in0=gate_tanh[chunk, pair][:], scalar=1.0, in1=diff[pair][:],
                 op0=ALU.add, op1=ALU.mult,
             )
+
+        def finish_blend(chunk, pair):
+            shape = [P, 2, CHUNK_WIDTHS[chunk]]
             result = blend.tile(shape, F32, name="result")
             nc.vector.scalar_tensor_tensor(
-                out=result[:], in0=gated[:], scalar=0.5, in1=mult_path[pair][:],
+                out=result[:], in0=gated[pair][:], scalar=0.5, in1=mult_path[pair][:],
                 op0=ALU.mult, op1=ALU.add,
             )
             nc.sync.dma_start(
@@ -284,15 +289,30 @@ def tile_nalu_kernel(tc, input_tensor, W_hat, M_hat, gate_words, gate_scales, ou
         multiply_gate(1)
 
         for chunk in range(CHUNKS):
-            for g in range(PASSES):
-                pair = g - (PASSES - PAIRS)
-                weave = chunk > 0 and pair >= 0
-                make_twice_w(chunk, g)
-                if weave:
-                    start_blend(chunk - 1, pair)
-                quantise_w(chunk, g)
-                if weave:
-                    finish_blend(chunk - 1, pair)
+            before = chunk - 1
+            make_twice_w(chunk, 0)
+            if chunk > 1:
+                finish_blend(chunk - 2, 1)
+            make_twice_w(chunk, 1)
+            quantise_w(chunk, 0)
+            if chunk > 0:
+                exponentiate(before, 0)
+            make_twice_w(chunk, 2)
+            if chunk > 0:
+                start_blend(before, 0)
+            quantise_w(chunk, 1)
+            if chunk > 0:
+                apply_gate(before, 0)
+                exponentiate(before, 1)
+            make_twice_w(chunk, 3)
+            if chunk > 0:
+                finish_blend(before, 0)
+            quantise_w(chunk, 2)
+            if chunk > 0:
+                start_blend(before, 1)
+            quantise_w(chunk, 3)
+            if chunk > 0:
+                apply_gate(before, 1)
             for pair in range(PAIRS):
                 squash_gate(chunk, pair)
             multiply_w(chunk)
@@ -303,6 +323,12 @@ def tile_nalu_kernel(tc, input_tensor, W_hat, M_hat, gate_words, gate_scales, ou
             if chunk_end % SLAB == 0 and next_slab < SLABS:
                 load_slab(next_slab)
                 load_gate_slab(next_slab)
+        finish_blend(CHUNKS - 2, 1)
+        for pair in range(PAIRS):
+            exponentiate(CHUNKS - 1, pair)
         for pair in range(PAIRS):
             start_blend(CHUNKS - 1, pair)
+        for pair in range(PAIRS):
+            apply_gate(CHUNKS - 1, pair)
+        for pair in range(PAIRS):
             finish_blend(CHUNKS - 1, pair)

@@ -217,15 +217,15 @@ def tile_nalu_kernel(tc, input_tensor, W_hat, M_hat, gate_words, gate_scales, ou
 
         def multiply_w(chunk):
             for pair in range(PAIRS):
-                log_sums[pair] = psum.tile([P, 2, CHUNK_WIDTHS[chunk]], F32, name="log_sums")
+                log_sums[chunk, pair] = psum.tile([P, 2, CHUNK_WIDTHS[chunk]], F32, name="log_sums")
                 multiply(
-                    log_sums[pair], pair, log_codes, log_scales,
+                    log_sums[chunk, pair], pair, log_codes, log_scales,
                     lambda g: w_codes[chunk][:, g, :],
                     lambda g: w_scales[chunk][:, g, :],
                 )
-                add_sums[pair] = psum.tile([P, 2, CHUNK_WIDTHS[chunk]], F32, name="add_sums")
+                add_sums[chunk, pair] = psum.tile([P, 2, CHUNK_WIDTHS[chunk]], F32, name="add_sums")
                 multiply(
-                    add_sums[pair], pair, x_codes, x_scales,
+                    add_sums[chunk, pair], pair, x_codes, x_scales,
                     lambda g: w_codes[chunk][:, g, :],
                     lambda g: w_scales[chunk][:, g, :],
                 )
@@ -241,29 +241,29 @@ def tile_nalu_kernel(tc, input_tensor, W_hat, M_hat, gate_words, gate_scales, ou
             )
 
         def exponentiate(chunk, pair):
-            mult_path[pair] = blend.tile([P, 2, CHUNK_WIDTHS[chunk]], F32, name="mult_path")
-            nc.scalar.activation(out=mult_path[pair][:], in_=log_sums[pair][:], func=ACT.Exp, scale=0.5)
+            mult_path[chunk, pair] = blend.tile([P, 2, CHUNK_WIDTHS[chunk]], F32, name="mult_path", bufs=3)
+            nc.scalar.activation(out=mult_path[chunk, pair][:], in_=log_sums[chunk, pair][:], func=ACT.Exp, scale=0.5)
 
         def start_blend(chunk, pair):
             shape = [P, 2, CHUNK_WIDTHS[chunk]]
-            diff[pair] = blend.tile(shape, F32, name="diff")
+            diff[chunk, pair] = blend.tile(shape, F32, name="diff")
             nc.vector.scalar_tensor_tensor(
-                out=diff[pair][:], in0=add_sums[pair][:], scalar=0.5, in1=mult_path[pair][:],
+                out=diff[chunk, pair][:], in0=add_sums[chunk, pair][:], scalar=0.5, in1=mult_path[chunk, pair][:],
                 op0=ALU.mult, op1=ALU.subtract,
             )
 
         def apply_gate(chunk, pair):
-            gated[pair] = blend.tile([P, 2, CHUNK_WIDTHS[chunk]], F32, name="gated")
+            gated[chunk, pair] = blend.tile([P, 2, CHUNK_WIDTHS[chunk]], F32, name="gated")
             nc.vector.scalar_tensor_tensor(
-                out=gated[pair][:], in0=gate_tanh[chunk, pair][:], scalar=1.0, in1=diff[pair][:],
+                out=gated[chunk, pair][:], in0=gate_tanh[chunk, pair][:], scalar=1.0, in1=diff[chunk, pair][:],
                 op0=ALU.add, op1=ALU.mult,
             )
 
         def finish_blend(chunk, pair):
             shape = [P, 2, CHUNK_WIDTHS[chunk]]
-            result = blend.tile(shape, F32, name="result")
+            result = blend.tile(shape, F32, name="result", bufs=4)
             nc.vector.scalar_tensor_tensor(
-                out=result[:], in0=gated[pair][:], scalar=0.5, in1=mult_path[pair][:],
+                out=result[:], in0=gated[chunk, pair][:], scalar=0.5, in1=mult_path[chunk, pair][:],
                 op0=ALU.mult, op1=ALU.add,
             )
             nc.sync.dma_start(
@@ -291,44 +291,52 @@ def tile_nalu_kernel(tc, input_tensor, W_hat, M_hat, gate_words, gate_scales, ou
         for chunk in range(CHUNKS):
             before = chunk - 1
             make_twice_w(chunk, 0)
+            if chunk > 0:
+                squash_gate(before, 0)
+            if chunk > 1:
+                apply_gate(chunk - 2, 1)
+            quantise_w(chunk, 0)
+
+            make_twice_w(chunk, 1)
+            if chunk > 0:
+                squash_gate(before, 1)
             if chunk > 1:
                 finish_blend(chunk - 2, 1)
-            make_twice_w(chunk, 1)
-            quantise_w(chunk, 0)
-            if chunk > 0:
-                exponentiate(before, 0)
+            quantise_w(chunk, 1)
+            if 0 < chunk < CHUNKS - 1:
+                multiply_gate(chunk + 1)
+
             make_twice_w(chunk, 2)
             if chunk > 0:
+                exponentiate(before, 0)
                 start_blend(before, 0)
-            quantise_w(chunk, 1)
-            if chunk > 0:
-                apply_gate(before, 0)
-                exponentiate(before, 1)
-            make_twice_w(chunk, 3)
-            if chunk > 0:
-                finish_blend(before, 0)
             quantise_w(chunk, 2)
             if chunk > 0:
-                start_blend(before, 1)
+                apply_gate(before, 0)
+
+            make_twice_w(chunk, 3)
+            if chunk > 0:
+                exponentiate(before, 1)
+                finish_blend(before, 0)
             quantise_w(chunk, 3)
             if chunk > 0:
-                apply_gate(before, 1)
-            for pair in range(PAIRS):
-                squash_gate(chunk, pair)
+                start_blend(before, 1)
             multiply_w(chunk)
-            if chunk + 2 < CHUNKS:
-                multiply_gate(chunk + 2)
             chunk_end = CHUNK_STARTS[chunk] + CHUNK_WIDTHS[chunk]
             next_slab = chunk_end // SLAB + 1
             if chunk_end % SLAB == 0 and next_slab < SLABS:
                 load_slab(next_slab)
                 load_gate_slab(next_slab)
-        finish_blend(CHUNKS - 2, 1)
+        last = CHUNKS - 1
         for pair in range(PAIRS):
-            exponentiate(CHUNKS - 1, pair)
+            squash_gate(last, pair)
+        apply_gate(last - 1, 1)
         for pair in range(PAIRS):
-            start_blend(CHUNKS - 1, pair)
+            exponentiate(last, pair)
+        finish_blend(last - 1, 1)
         for pair in range(PAIRS):
-            apply_gate(CHUNKS - 1, pair)
+            start_blend(last, pair)
         for pair in range(PAIRS):
-            finish_blend(CHUNKS - 1, pair)
+            apply_gate(last, pair)
+        for pair in range(PAIRS):
+            finish_blend(last, pair)

@@ -22,10 +22,14 @@ K_PASS = P * PACK
 PASSES = IN // K_PASS
 ROW_TILES = B // P
 PAIRS = ROW_TILES // 2
+BANK = 512
 CHUNK = 256
 CHUNK_WIDTHS = [CHUNK] * (OUT // CHUNK - 1) + [CHUNK // 2] * 2
 CHUNK_STARTS = [sum(CHUNK_WIDTHS[:c]) for c in range(len(CHUNK_WIDTHS))]
 CHUNKS = len(CHUNK_WIDTHS)
+LAST = CHUNKS - 1
+SHARE = [BANK // width for width in CHUNK_WIDTHS]
+PARTS = [range(ROW_TILES // share) for share in SHARE]
 SLAB = 2 * CHUNK
 SLABS = OUT // SLAB
 X_UNITS = 2 * ROW_TILES
@@ -184,19 +188,17 @@ def tile_nalu_kernel(tc, input_tensor, W_hat, M_hat, gate_words, gate_scales, ou
                 in_=w_grouped[g][:].rearrange("p n j -> p (n j)"),
             )
 
-        def multiply(bank, pair, lhs_codes, lhs_scales, rhs_of_pass, rhs_scale_of_pass):
-            for i in range(2):
-                row_tile = 2 * pair + i
-                for g in range(PASSES):
-                    nc.tensor.matmul_mx(
-                        out=bank[:, i, :],
-                        lhsT=lhs_codes[:, row_tile, g, :].bitcast(FP8X4),
-                        lhsT_scale=lhs_scales[:, row_tile, g, :],
-                        rhs=rhs_of_pass(g).bitcast(FP8X4),
-                        rhs_scale=rhs_scale_of_pass(g),
-                        start=(g == 0),
-                        stop=(g == PASSES - 1),
-                    )
+        def multiply(bank, row_tile, lhs_codes, lhs_scales, rhs_of_pass, rhs_scale_of_pass, passes):
+            for g in passes:
+                nc.tensor.matmul_mx(
+                    out=bank,
+                    lhsT=lhs_codes[:, row_tile, g, :].bitcast(FP8X4),
+                    lhsT_scale=lhs_scales[:, row_tile, g, :],
+                    rhs=rhs_of_pass(g).bitcast(FP8X4),
+                    rhs_scale=rhs_scale_of_pass(g),
+                    start=(g == 0),
+                    stop=(g == PASSES - 1),
+                )
 
         gate_sums = {}
         log_sums = {}
@@ -205,71 +207,92 @@ def tile_nalu_kernel(tc, input_tensor, W_hat, M_hat, gate_words, gate_scales, ou
 
         def multiply_gate(chunk):
             slab, cols = columns_in_slab(chunk)
-            for pair in range(PAIRS):
-                gate_sums[chunk, pair] = psum.tile(
-                    [P, 2, CHUNK_WIDTHS[chunk]], F32, name="gate_sums", tag=EARLY_BANKS, bufs=4
+            for part in PARTS[chunk]:
+                gate_sums[chunk, part] = psum.tile(
+                    [P, SHARE[chunk], CHUNK_WIDTHS[chunk]], F32, name="gate_sums", tag=EARLY_BANKS, bufs=4
                 )
-                multiply(
-                    gate_sums[chunk, pair], pair, x_codes, x_scales,
-                    lambda g: gate_slabs[slab][:, g, cols],
-                    lambda g: gate_planes[4 * g : P, columns(chunk)],
-                )
+                for i in range(SHARE[chunk]):
+                    multiply(
+                        gate_sums[chunk, part][:, i, :], SHARE[chunk] * part + i, x_codes, x_scales,
+                        lambda g: gate_slabs[slab][:, g, cols],
+                        lambda g: gate_planes[4 * g : P, columns(chunk)],
+                        range(PASSES),
+                    )
+
+        def multiply_by_w(bank, row_tile, lhs_codes, lhs_scales, chunk, passes):
+            multiply(
+                bank, row_tile, lhs_codes, lhs_scales,
+                lambda g: w_codes[chunk][:, g, :],
+                lambda g: w_scales[chunk][:, g, :],
+                passes,
+            )
 
         def multiply_w(chunk):
-            for pair in range(PAIRS):
-                log_sums[chunk, pair] = psum.tile([P, 2, CHUNK_WIDTHS[chunk]], F32, name="log_sums")
-                multiply(
-                    log_sums[chunk, pair], pair, log_codes, log_scales,
-                    lambda g: w_codes[chunk][:, g, :],
-                    lambda g: w_scales[chunk][:, g, :],
-                )
-                add_sums[chunk, pair] = psum.tile([P, 2, CHUNK_WIDTHS[chunk]], F32, name="add_sums")
-                multiply(
-                    add_sums[chunk, pair], pair, x_codes, x_scales,
-                    lambda g: w_codes[chunk][:, g, :],
-                    lambda g: w_scales[chunk][:, g, :],
-                )
+            shape = [P, SHARE[chunk], CHUNK_WIDTHS[chunk]]
+            for part in PARTS[chunk]:
+                first = SHARE[chunk] * part
+                log_sums[chunk, part] = psum.tile(shape, F32, name="log_sums")
+                for i in range(SHARE[chunk]):
+                    multiply_by_w(log_sums[chunk, part][:, i, :], first + i, log_codes, log_scales, chunk, range(PASSES))
+                add_sums[chunk, part] = psum.tile(shape, F32, name="add_sums")
+                for i in range(SHARE[chunk]):
+                    multiply_by_w(add_sums[chunk, part][:, i, :], first + i, x_codes, x_scales, chunk, range(PASSES))
+
+        last_log = {}
+        last_add = {}
+
+        def open_last(row_tile, sums, name):
+            tag = name if row_tile < 2 else EARLY_BANKS
+            sums[row_tile] = psum.tile([P, CHUNK_WIDTHS[LAST]], F32, name="last_" + name, tag=tag, bufs=2 if row_tile < 2 else 4)
 
         mult_path = {}
         diff = {}
         gated = {}
 
-        def squash_gate(chunk, pair):
-            gate_tanh[chunk, pair] = stream.tile([P, 2, CHUNK_WIDTHS[chunk]], F32, name="gate_tanh", bufs=4)
+        def squash_gate(chunk, part):
+            gate_tanh[chunk, part] = stream.tile([P, SHARE[chunk], CHUNK_WIDTHS[chunk]], F32, name="gate_tanh", bufs=4)
             nc.scalar.activation(
-                out=gate_tanh[chunk, pair][:], in_=gate_sums[chunk, pair][:], func=ACT.Tanh, scale=0.5
+                out=gate_tanh[chunk, part][:], in_=gate_sums[chunk, part][:], func=ACT.Tanh, scale=0.5
             )
 
-        def exponentiate(chunk, pair):
-            mult_path[chunk, pair] = blend.tile([P, 2, CHUNK_WIDTHS[chunk]], F32, name="mult_path", bufs=3)
-            nc.scalar.activation(out=mult_path[chunk, pair][:], in_=log_sums[chunk, pair][:], func=ACT.Exp, scale=0.5)
+        def exponentiate(chunk, part):
+            mult_path[chunk, part] = blend.tile([P, SHARE[chunk], CHUNK_WIDTHS[chunk]], F32, name="mult_path", bufs=3)
+            nc.scalar.activation(out=mult_path[chunk, part][:], in_=log_sums[chunk, part][:], func=ACT.Exp, scale=0.5)
 
-        def start_blend(chunk, pair):
-            shape = [P, 2, CHUNK_WIDTHS[chunk]]
-            diff[chunk, pair] = blend.tile(shape, F32, name="diff")
+        def start_blend(chunk, part):
+            shape = [P, SHARE[chunk], CHUNK_WIDTHS[chunk]]
+            diff[chunk, part] = blend.tile(shape, F32, name="diff")
             nc.vector.scalar_tensor_tensor(
-                out=diff[chunk, pair][:], in0=add_sums[chunk, pair][:], scalar=0.5, in1=mult_path[chunk, pair][:],
+                out=diff[chunk, part][:], in0=add_sums[chunk, part][:], scalar=0.5, in1=mult_path[chunk, part][:],
                 op0=ALU.mult, op1=ALU.subtract,
             )
 
+        def rows_of_pair(chunk, pair):
+            part, first = divmod(2 * pair, SHARE[chunk])
+            return part, slice(first, first + 2)
+
         def apply_gate(chunk, pair):
+            part, rows = rows_of_pair(chunk, pair)
             gated[chunk, pair] = blend.tile([P, 2, CHUNK_WIDTHS[chunk]], F32, name="gated")
             nc.vector.scalar_tensor_tensor(
-                out=gated[chunk, pair][:], in0=gate_tanh[chunk, pair][:], scalar=1.0, in1=diff[chunk, pair][:],
-                op0=ALU.add, op1=ALU.mult,
+                out=gated[chunk, pair][:], in0=gate_tanh[chunk, part][:, rows, :], scalar=1.0,
+                in1=diff[chunk, part][:, rows, :], op0=ALU.add, op1=ALU.mult,
             )
 
-        def finish_blend(chunk, pair):
-            shape = [P, 2, CHUNK_WIDTHS[chunk]]
-            result = blend.tile(shape, F32, name="result", bufs=4)
-            nc.vector.scalar_tensor_tensor(
-                out=result[:], in0=gated[chunk, pair][:], scalar=0.5, in1=mult_path[chunk, pair][:],
-                op0=ALU.mult, op1=ALU.add,
-            )
+        def store(chunk, pair, result):
             nc.sync.dma_start(
                 out=out[2 * P * pair : 2 * P * (pair + 1), columns(chunk)].rearrange("(i p) n -> p i n", p=P),
                 in_=result[:],
             )
+
+        def finish_blend(chunk, pair):
+            part, rows = rows_of_pair(chunk, pair)
+            result = blend.tile([P, 2, CHUNK_WIDTHS[chunk]], F32, name="result", bufs=4)
+            nc.vector.scalar_tensor_tensor(
+                out=result[:], in0=gated[chunk, pair][:], scalar=0.5, in1=mult_path[chunk, part][:, rows, :],
+                op0=ALU.mult, op1=ALU.add,
+            )
+            store(chunk, pair, result)
 
         for unit in range(X_UNITS):
             load_x(unit)
@@ -290,53 +313,90 @@ def tile_nalu_kernel(tc, input_tensor, W_hat, M_hat, gate_words, gate_scales, ou
 
         for chunk in range(CHUNKS):
             before = chunk - 1
+            parts = PARTS[before] if chunk > 0 else range(0)
+            leftovers = PARTS[chunk - 2][1:] if chunk > 1 else range(0)
             make_twice_w(chunk, 0)
-            if chunk > 0:
-                squash_gate(before, 0)
-            if chunk > 1:
-                apply_gate(chunk - 2, 1)
+            for part in parts[:1]:
+                squash_gate(before, part)
+            for part in leftovers:
+                apply_gate(chunk - 2, part)
             quantise_w(chunk, 0)
 
             make_twice_w(chunk, 1)
-            if chunk > 0:
-                squash_gate(before, 1)
-            if chunk > 1:
-                finish_blend(chunk - 2, 1)
+            for part in parts[1:]:
+                squash_gate(before, part)
+            for part in leftovers:
+                finish_blend(chunk - 2, part)
             quantise_w(chunk, 1)
-            if 0 < chunk < CHUNKS - 1:
+            if 0 < chunk < LAST:
                 multiply_gate(chunk + 1)
 
             make_twice_w(chunk, 2)
-            if chunk > 0:
-                exponentiate(before, 0)
-                start_blend(before, 0)
+            for part in parts[:1]:
+                exponentiate(before, part)
+                start_blend(before, part)
             quantise_w(chunk, 2)
-            if chunk > 0:
+            if 0 < chunk < LAST:
                 apply_gate(before, 0)
+            if chunk == LAST:
+                for row_tile in (2, 3, 0, 1):
+                    open_last(row_tile, last_log, "log_sums")
+                    multiply_by_w(last_log[row_tile][:], row_tile, log_codes, log_scales, LAST, range(3))
+                for row_tile in (2, 0, 1):
+                    open_last(row_tile, last_add, "add_sums")
+                    multiply_by_w(last_add[row_tile][:], row_tile, x_codes, x_scales, LAST, range(3))
 
             make_twice_w(chunk, 3)
-            if chunk > 0:
-                exponentiate(before, 1)
+            for part in parts[1:]:
+                exponentiate(before, part)
+            if chunk == LAST:
+                apply_gate(before, 0)
+            elif chunk > 0:
                 finish_blend(before, 0)
             quantise_w(chunk, 3)
-            if chunk > 0:
-                start_blend(before, 1)
-            multiply_w(chunk)
+            for part in parts[1:]:
+                start_blend(before, part)
+            if chunk < LAST:
+                multiply_w(chunk)
             chunk_end = CHUNK_STARTS[chunk] + CHUNK_WIDTHS[chunk]
             next_slab = chunk_end // SLAB + 1
             if chunk_end % SLAB == 0 and next_slab < SLABS:
                 load_slab(next_slab)
                 load_gate_slab(next_slab)
-        last = CHUNKS - 1
+
+        width = CHUNK_WIDTHS[LAST]
+        squash_gate(LAST, 0)
+        open_last(ROW_TILES - 1, last_add, "add_sums")
+        for row_tile in range(ROW_TILES):
+            multiply_by_w(last_log[row_tile][:], row_tile, log_codes, log_scales, LAST, range(3, 4))
+            done = 0 if row_tile == ROW_TILES - 1 else 3
+            multiply_by_w(last_add[row_tile][:], row_tile, x_codes, x_scales, LAST, range(done, 4))
+        apply_gate(LAST - 1, 1)
         for pair in range(PAIRS):
-            squash_gate(last, pair)
-        apply_gate(last - 1, 1)
+            finish_blend(LAST - 1, pair)
+        one_minus_g = blend.tile([P, ROW_TILES, width], F32, name="one_minus_g", bufs=1)
+        nc.vector.tensor_scalar(
+            out=one_minus_g[:], in0=gate_tanh[LAST, 0][:], scalar1=-0.5, scalar2=0.5, op0=ALU.mult, op1=ALU.add
+        )
+        last_m = blend.tile([P, ROW_TILES, width], F32, name="mult_path", bufs=3)
+        gated_a = blend.tile([P, ROW_TILES, width], F32, name="gated")
+        gated_m = blend.tile([P, ROW_TILES, width], F32, name="diff")
+        for row_tile in range(ROW_TILES):
+            nc.scalar.activation(out=last_m[:, row_tile, :], in_=last_log[row_tile][:], func=ACT.Exp, scale=0.5)
+            nc.vector.scalar_tensor_tensor(
+                out=gated_a[:, row_tile, :], in0=gate_tanh[LAST, 0][:, row_tile, :], scalar=1.0,
+                in1=last_add[row_tile][:], op0=ALU.add, op1=ALU.mult,
+            )
         for pair in range(PAIRS):
-            exponentiate(last, pair)
-        finish_blend(last - 1, 1)
+            rows = slice(2 * pair, 2 * pair + 2)
+            nc.vector.tensor_tensor(
+                out=gated_m[:, rows, :], in0=one_minus_g[:, rows, :], in1=last_m[:, rows, :], op=ALU.mult
+            )
         for pair in range(PAIRS):
-            start_blend(last, pair)
-        for pair in range(PAIRS):
-            apply_gate(last, pair)
-        for pair in range(PAIRS):
-            finish_blend(last, pair)
+            rows = slice(2 * pair, 2 * pair + 2)
+            result = blend.tile([P, 2, width], F32, name="result", bufs=4)
+            nc.vector.scalar_tensor_tensor(
+                out=result[:], in0=gated_a[:, rows, :], scalar=0.25, in1=gated_m[:, rows, :],
+                op0=ALU.mult, op1=ALU.add,
+            )
+            store(LAST, pair, result)

@@ -32,9 +32,12 @@ SHARE = [BANK // width for width in CHUNK_WIDTHS]
 PARTS = [range(ROW_TILES // share) for share in SHARE]
 SLAB = 2 * CHUNK
 SLABS = OUT // SLAB
-X_UNITS = 2 * ROW_TILES
-UNIT_K = 2 * K_PASS
+X_UNITS = [(0, range(0, 1)), (0, range(1, 2)), (0, range(2, 4))] + [
+    (row_tile, range(2 * half, 2 * half + 2)) for row_tile in range(1, ROW_TILES) for half in range(2)
+]
 EARLY_BANKS = "x_t_then_gate_sums"
+EARLY_SUMS = [("log_sums", 2), ("log_sums", 3), ("add_sums", 2), ("log_sums", 0), ("add_sums", 0)]
+LATE_SUMS = [("log_sums", 1), ("add_sums", 1)]
 ABS_MASK = 0x7FFF7FFF
 
 
@@ -42,7 +45,7 @@ def tile_nalu_kernel(tc, input_tensor, W_hat, M_hat, gate_words, gate_scales, ou
     nc = tc.nc
     with ExitStack() as stack:
         keep = stack.enter_context(tc.tile_pool(name="keep", bufs=1))
-        x_pool = stack.enter_context(tc.tile_pool(name="x_pool", bufs=X_UNITS))
+        x_pool = stack.enter_context(tc.tile_pool(name="x_pool", bufs=1))
         slabs = stack.enter_context(tc.tile_pool(name="slabs", bufs=2))
         stream = stack.enter_context(tc.tile_pool(name="stream", bufs=3))
         blend = stack.enter_context(tc.tile_pool(name="blend", bufs=2))
@@ -62,12 +65,17 @@ def tile_nalu_kernel(tc, input_tensor, W_hat, M_hat, gate_words, gate_scales, ou
 
         x_rows = {}
 
+        def unit_tile(unit, name):
+            size = len(unit[1])
+            count = sum(len(passes) == size for tile_of_rows, passes in X_UNITS)
+            return x_pool.tile([P, size * K_PASS], BF16, name=name, tag="%s_%d" % (name, size), bufs=count, align_bytes=64)
+
         def load_x(unit):
-            row_tile, half = divmod(unit, 2)
-            x_rows[unit] = x_pool.tile([P, UNIT_K], BF16, name="x_rows")
+            row_tile, passes = unit
+            x_rows[unit] = unit_tile(unit, "x_rows")
             nc.sync.dma_start(
                 out=x_rows[unit][:],
-                in_=input_tensor[P * row_tile : P * (row_tile + 1), UNIT_K * half : UNIT_K * (half + 1)],
+                in_=input_tensor[P * row_tile : P * (row_tile + 1), K_PASS * passes.start : K_PASS * passes.stop],
             )
 
         def load_gate_planes():
@@ -114,19 +122,20 @@ def tile_nalu_kernel(tc, input_tensor, W_hat, M_hat, gate_words, gate_scales, ou
         log_grouped = {}
 
         def prepare_x(unit):
+            size = len(unit[1])
             words = x_rows[unit][:].bitcast(F32)
-            x_t = psum.tile([P, 2, 2, P], F32, name="x_t", tag=EARLY_BANKS, bufs=4)
-            for g in range(2):
+            x_t = psum.tile([P, size, 2, P], F32, name="x_t", tag=EARLY_BANKS, bufs=4)
+            for g in range(size):
                 for w in range(2):
                     nc.tensor.transpose(
                         x_t[:, g, w, :], words[:, 256 * g + w : 256 * (g + 1) : 2], identity[:]
                     )
-            x_grouped[unit] = x_pool.tile([P, UNIT_K], BF16, name="x_grouped", align_bytes=64)
+            x_grouped[unit] = unit_tile(unit, "x_grouped")
             nc.vector.tensor_copy(
-                out=x_grouped[unit][:].bitcast(F32).rearrange("p (g r w) -> p g r w", g=2, w=2),
+                out=x_grouped[unit][:].bitcast(F32).rearrange("p (g r w) -> p g r w", g=size, w=2),
                 in_=x_t[:].rearrange("p g w r -> p g r w"),
             )
-            x_abs = stream.tile([P, UNIT_K], BF16, name="x_abs")
+            x_abs = stream.tile([P, size * K_PASS], BF16, name="x_abs")
             nc.vector.tensor_scalar(
                 out=x_abs[:].bitcast(I32),
                 in0=x_grouped[unit][:].bitcast(I32),
@@ -134,12 +143,11 @@ def tile_nalu_kernel(tc, input_tensor, W_hat, M_hat, gate_words, gate_scales, ou
                 scalar2=None,
                 op0=ALU.bitwise_and,
             )
-            log_grouped[unit] = x_pool.tile([P, UNIT_K], BF16, name="log_grouped", align_bytes=64)
+            log_grouped[unit] = unit_tile(unit, "log_grouped")
             nc.scalar.activation(out=log_grouped[unit][:], in_=x_abs[:], func=ACT.Ln, bias=EPS, scale=1.0)
 
         def quantise_unit(grouped, codes, scales, unit):
-            row_tile, half = divmod(unit, 2)
-            passes = slice(2 * half, 2 * half + 2)
+            row_tile, passes = unit[0], slice(unit[1].start, unit[1].stop)
             nc.vector.quantize_mx(
                 out=codes[:, row_tile, passes, :].rearrange("p g r -> p (g r)").bitcast(FP8X4),
                 scales=scales[:, row_tile, passes, :].rearrange("p g r -> p (g r)"),
@@ -238,12 +246,15 @@ def tile_nalu_kernel(tc, input_tensor, W_hat, M_hat, gate_words, gate_scales, ou
                 for i in range(SHARE[chunk]):
                     multiply_by_w(add_sums[chunk, part][:, i, :], first + i, x_codes, x_scales, chunk, range(PASSES))
 
-        last_log = {}
-        last_add = {}
+        last_sums = {}
 
-        def open_last(row_tile, sums, name):
-            tag = name if row_tile < 2 else EARLY_BANKS
-            sums[row_tile] = psum.tile([P, CHUNK_WIDTHS[LAST]], F32, name="last_" + name, tag=tag, bufs=2 if row_tile < 2 else 4)
+        def open_last(sums, row_tile):
+            tag, bufs = (EARLY_BANKS, 4) if row_tile >= 2 else (sums, 2)
+            last_sums[sums, row_tile] = psum.tile([P, CHUNK_WIDTHS[LAST]], F32, name="last_sums", tag=tag, bufs=bufs)
+
+        def multiply_last(sums, row_tile, passes):
+            codes, scales = (log_codes, log_scales) if sums == "log_sums" else (x_codes, x_scales)
+            multiply_by_w(last_sums[sums, row_tile][:], row_tile, codes, scales, LAST, passes)
 
         mult_path = {}
         diff = {}
@@ -294,7 +305,7 @@ def tile_nalu_kernel(tc, input_tensor, W_hat, M_hat, gate_words, gate_scales, ou
             )
             store(chunk, pair, result)
 
-        for unit in range(X_UNITS):
+        for unit in X_UNITS:
             load_x(unit)
         load_gate_planes()
         load_slab(0)
@@ -302,11 +313,11 @@ def tile_nalu_kernel(tc, input_tensor, W_hat, M_hat, gate_words, gate_scales, ou
         load_slab(1)
         load_gate_slab(1)
 
-        for unit in range(X_UNITS):
+        for unit in X_UNITS:
             prepare_x(unit)
-        for unit in range(X_UNITS):
+        for unit in X_UNITS:
             quantise_unit(x_grouped, x_codes, x_scales, unit)
-        for unit in range(X_UNITS):
+        for unit in X_UNITS:
             quantise_unit(log_grouped, log_codes, log_scales, unit)
         multiply_gate(0)
         multiply_gate(1)
@@ -330,6 +341,10 @@ def tile_nalu_kernel(tc, input_tensor, W_hat, M_hat, gate_words, gate_scales, ou
             quantise_w(chunk, 1)
             if 0 < chunk < LAST:
                 multiply_gate(chunk + 1)
+            if chunk == LAST:
+                for sums, row_tile in EARLY_SUMS:
+                    open_last(sums, row_tile)
+                    multiply_last(sums, row_tile, range(2))
 
             make_twice_w(chunk, 2)
             for part in parts[:1]:
@@ -339,12 +354,11 @@ def tile_nalu_kernel(tc, input_tensor, W_hat, M_hat, gate_words, gate_scales, ou
             if 0 < chunk < LAST:
                 apply_gate(before, 0)
             if chunk == LAST:
-                for row_tile in (2, 3, 0, 1):
-                    open_last(row_tile, last_log, "log_sums")
-                    multiply_by_w(last_log[row_tile][:], row_tile, log_codes, log_scales, LAST, range(3))
-                for row_tile in (2, 0, 1):
-                    open_last(row_tile, last_add, "add_sums")
-                    multiply_by_w(last_add[row_tile][:], row_tile, x_codes, x_scales, LAST, range(3))
+                for sums, row_tile in LATE_SUMS:
+                    open_last(sums, row_tile)
+                    multiply_last(sums, row_tile, range(2))
+                for sums, row_tile in EARLY_SUMS + LATE_SUMS:
+                    multiply_last(sums, row_tile, range(2, 3))
 
             make_twice_w(chunk, 3)
             for part in parts[1:]:
@@ -366,26 +380,23 @@ def tile_nalu_kernel(tc, input_tensor, W_hat, M_hat, gate_words, gate_scales, ou
 
         width = CHUNK_WIDTHS[LAST]
         squash_gate(LAST, 0)
-        open_last(ROW_TILES - 1, last_add, "add_sums")
+        one_minus_g = blend.tile([P, ROW_TILES, width], F32, name="one_minus_g", bufs=1)
+        nc.scalar.activation(out=one_minus_g[:], in_=gate_tanh[LAST, 0][:], func=ACT.Identity, scale=-0.5, bias=0.5)
+        open_last("add_sums", ROW_TILES - 1)
         for row_tile in range(ROW_TILES):
-            multiply_by_w(last_log[row_tile][:], row_tile, log_codes, log_scales, LAST, range(3, 4))
-            done = 0 if row_tile == ROW_TILES - 1 else 3
-            multiply_by_w(last_add[row_tile][:], row_tile, x_codes, x_scales, LAST, range(done, 4))
+            multiply_last("log_sums", row_tile, range(3, 4))
+            multiply_last("add_sums", row_tile, range(0 if row_tile == ROW_TILES - 1 else 3, 4))
         apply_gate(LAST - 1, 1)
         for pair in range(PAIRS):
             finish_blend(LAST - 1, pair)
-        one_minus_g = blend.tile([P, ROW_TILES, width], F32, name="one_minus_g", bufs=1)
-        nc.vector.tensor_scalar(
-            out=one_minus_g[:], in0=gate_tanh[LAST, 0][:], scalar1=-0.5, scalar2=0.5, op0=ALU.mult, op1=ALU.add
-        )
         last_m = blend.tile([P, ROW_TILES, width], F32, name="mult_path", bufs=3)
         gated_a = blend.tile([P, ROW_TILES, width], F32, name="gated")
         gated_m = blend.tile([P, ROW_TILES, width], F32, name="diff")
         for row_tile in range(ROW_TILES):
-            nc.scalar.activation(out=last_m[:, row_tile, :], in_=last_log[row_tile][:], func=ACT.Exp, scale=0.5)
+            nc.scalar.activation(out=last_m[:, row_tile, :], in_=last_sums["log_sums", row_tile][:], func=ACT.Exp, scale=0.5)
             nc.vector.scalar_tensor_tensor(
                 out=gated_a[:, row_tile, :], in0=gate_tanh[LAST, 0][:, row_tile, :], scalar=1.0,
-                in1=last_add[row_tile][:], op0=ALU.add, op1=ALU.mult,
+                in1=last_sums["add_sums", row_tile][:], op0=ALU.add, op1=ALU.mult,
             )
         for pair in range(PAIRS):
             rows = slice(2 * pair, 2 * pair + 2)

@@ -36,6 +36,7 @@ X_UNITS = [(0, range(0, 1)), (0, range(1, 2)), (0, range(2, 4))] + [
     (row_tile, range(2 * half, 2 * half + 2)) for row_tile in range(1, ROW_TILES) for half in range(2)
 ]
 EARLY_BANKS = "x_t_then_gate_sums"
+LATE_BANKS = ["log_sums", "add_sums"]
 EARLY_SUMS = [("log_sums", 2), ("log_sums", 3), ("add_sums", 2), ("log_sums", 0), ("add_sums", 0)]
 LATE_SUMS = [("log_sums", 1), ("add_sums", 1)]
 ABS_MASK = 0x7FFF7FFF
@@ -118,33 +119,56 @@ def tile_nalu_kernel(tc, input_tensor, W_hat, M_hat, gate_words, gate_scales, ou
         def columns(chunk):
             return slice(CHUNK_STARTS[chunk], CHUNK_STARTS[chunk] + CHUNK_WIDTHS[chunk])
 
+        x_abs = {}
+        abs_t = {}
+        x_t = {}
         x_grouped = {}
         log_grouped = {}
 
-        def prepare_x(unit):
+        def clear_signs(unit):
             size = len(unit[1])
-            words = x_rows[unit][:].bitcast(F32)
-            x_t = psum.tile([P, size, 2, P], F32, name="x_t", tag=EARLY_BANKS, bufs=4)
-            for g in range(size):
-                for w in range(2):
-                    nc.tensor.transpose(
-                        x_t[:, g, w, :], words[:, 256 * g + w : 256 * (g + 1) : 2], identity[:]
-                    )
-            x_grouped[unit] = unit_tile(unit, "x_grouped")
-            nc.vector.tensor_copy(
-                out=x_grouped[unit][:].bitcast(F32).rearrange("p (g r w) -> p g r w", g=size, w=2),
-                in_=x_t[:].rearrange("p g w r -> p g r w"),
-            )
-            x_abs = stream.tile([P, size * K_PASS], BF16, name="x_abs")
+            x_abs[unit] = stream.tile([P, size, 2, P], I32, name="x_abs")
             nc.vector.tensor_scalar(
-                out=x_abs[:].bitcast(I32),
-                in0=x_grouped[unit][:].bitcast(I32),
+                out=x_abs[unit][:],
+                in0=x_rows[unit][:].bitcast(I32).rearrange("r (g p w) -> r g w p", g=size, w=2),
                 scalar1=ABS_MASK,
                 scalar2=None,
                 op0=ALU.bitwise_and,
             )
+
+        def transpose_abs(unit):
+            size = len(unit[1])
+            abs_t[unit] = psum.tile([P, size, 2, P], F32, name="abs_t", tag=LATE_BANKS[X_UNITS.index(unit) % 2])
+            for g in range(size):
+                for w in range(2):
+                    nc.tensor.transpose(abs_t[unit][:, g, w, :], x_abs[unit][:, g, w, :].bitcast(F32), identity[:])
+
+        def take_log(unit):
             log_grouped[unit] = unit_tile(unit, "log_grouped")
-            nc.scalar.activation(out=log_grouped[unit][:], in_=x_abs[:], func=ACT.Ln, bias=EPS, scale=1.0)
+            for g in range(len(unit[1])):
+                nc.scalar.activation(
+                    out=log_grouped[unit][:, K_PASS * g : K_PASS * (g + 1)].rearrange("p (r w e) -> p r w e", w=2, e=2),
+                    in_=abs_t[unit][:, g].bitcast(BF16).rearrange("p w (r e) -> p r w e", e=2),
+                    func=ACT.Ln, bias=EPS, scale=1.0,
+                )
+
+        def transpose_x(unit):
+            size = len(unit[1])
+            words = x_rows[unit][:].bitcast(F32)
+            x_t[unit] = psum.tile([P, size, 2, P], F32, name="x_t", tag=EARLY_BANKS, bufs=4)
+            for g in range(size):
+                for w in range(2):
+                    nc.tensor.transpose(
+                        x_t[unit][:, g, w, :], words[:, 256 * g + w : 256 * (g + 1) : 2], identity[:]
+                    )
+
+        def group_x(unit):
+            size = len(unit[1])
+            x_grouped[unit] = unit_tile(unit, "x_grouped")
+            nc.vector.tensor_copy(
+                out=x_grouped[unit][:].bitcast(F32).rearrange("p (g r w) -> p g r w", g=size, w=2),
+                in_=x_t[unit][:].rearrange("p g w r -> p g r w"),
+            )
 
         def quantise_unit(grouped, codes, scales, unit):
             row_tile, passes = unit[0], slice(unit[1].start, unit[1].stop)
@@ -313,8 +337,12 @@ def tile_nalu_kernel(tc, input_tensor, W_hat, M_hat, gate_words, gate_scales, ou
         load_slab(1)
         load_gate_slab(1)
 
-        for unit in X_UNITS:
-            prepare_x(unit)
+        steps = [(clear_signs, -1), (transpose_abs, 0), (take_log, 0), (transpose_x, 2), (group_x, 3)]
+        clear_signs(X_UNITS[0])
+        for i in range(len(X_UNITS) + 3):
+            for step, behind in steps:
+                if 0 <= i - behind < len(X_UNITS):
+                    step(X_UNITS[i - behind])
         for unit in X_UNITS:
             quantise_unit(x_grouped, x_codes, x_scales, unit)
         for unit in X_UNITS:

@@ -138,19 +138,18 @@ def tile_nalu_kernel(tc, input_tensor, W_hat, M_hat, gate_words, gate_scales, ou
 
         def transpose_abs(unit):
             size = len(unit[1])
-            abs_t[unit] = psum.tile([P, size, 2, P], F32, name="abs_t", tag=LATE_BANKS[X_UNITS.index(unit) % 2])
+            abs_t[unit] = psum.tile([P, 2, size, P], F32, name="abs_t", tag=LATE_BANKS[X_UNITS.index(unit) % 2])
             for g in range(size):
                 for w in range(2):
-                    nc.tensor.transpose(abs_t[unit][:, g, w, :], x_abs[unit][:, g, w, :].bitcast(F32), identity[:])
+                    nc.tensor.transpose(abs_t[unit][:, w, g, :], x_abs[unit][:, g, w, :].bitcast(F32), identity[:])
 
         def take_log(unit):
             log_grouped[unit] = unit_tile(unit, "log_grouped")
-            for g in range(len(unit[1])):
-                nc.scalar.activation(
-                    out=log_grouped[unit][:, K_PASS * g : K_PASS * (g + 1)].rearrange("p (r w e) -> p r w e", w=2, e=2),
-                    in_=abs_t[unit][:, g].bitcast(BF16).rearrange("p w (r e) -> p r w e", e=2),
-                    func=ACT.Ln, bias=EPS, scale=1.0,
-                )
+            nc.scalar.activation(
+                out=log_grouped[unit][:].rearrange("p (q w e) -> p q w e", w=2, e=2),
+                in_=abs_t[unit][:].bitcast(BF16).rearrange("p w g (r e) -> p (g r) w e", e=2),
+                func=ACT.Ln, bias=EPS, scale=1.0,
+            )
 
         def transpose_x(unit):
             size = len(unit[1])
@@ -259,13 +258,21 @@ def tile_nalu_kernel(tc, input_tensor, W_hat, M_hat, gate_words, gate_scales, ou
                 passes,
             )
 
+        def start_multiply_w(chunk):
+            log_sums[chunk, 0] = psum.tile([P, SHARE[chunk], CHUNK_WIDTHS[chunk]], F32, name="log_sums")
+            multiply_by_w(log_sums[chunk, 0][:, 0, :], 0, log_codes, log_scales, chunk, range(PASSES - 1))
+
         def multiply_w(chunk):
             shape = [P, SHARE[chunk], CHUNK_WIDTHS[chunk]]
             for part in PARTS[chunk]:
                 first = SHARE[chunk] * part
-                log_sums[chunk, part] = psum.tile(shape, F32, name="log_sums")
+                if part > 0:
+                    log_sums[chunk, part] = psum.tile(shape, F32, name="log_sums")
                 for i in range(SHARE[chunk]):
-                    multiply_by_w(log_sums[chunk, part][:, i, :], first + i, log_codes, log_scales, chunk, range(PASSES))
+                    done = PASSES - 1 if first + i == 0 else 0
+                    multiply_by_w(
+                        log_sums[chunk, part][:, i, :], first + i, log_codes, log_scales, chunk, range(done, PASSES)
+                    )
                 add_sums[chunk, part] = psum.tile(shape, F32, name="add_sums")
                 for i in range(SHARE[chunk]):
                     multiply_by_w(add_sums[chunk, part][:, i, :], first + i, x_codes, x_scales, chunk, range(PASSES))
@@ -331,8 +338,8 @@ def tile_nalu_kernel(tc, input_tensor, W_hat, M_hat, gate_words, gate_scales, ou
 
         for unit in X_UNITS:
             load_x(unit)
-        load_gate_planes()
         load_slab(0)
+        load_gate_planes()
         load_gate_slab(0)
         load_slab(1)
         load_gate_slab(1)
@@ -348,7 +355,6 @@ def tile_nalu_kernel(tc, input_tensor, W_hat, M_hat, gate_words, gate_scales, ou
         for unit in X_UNITS:
             quantise_unit(log_grouped, log_codes, log_scales, unit)
         multiply_gate(0)
-        multiply_gate(1)
 
         for chunk in range(CHUNKS):
             before = chunk - 1
@@ -367,8 +373,6 @@ def tile_nalu_kernel(tc, input_tensor, W_hat, M_hat, gate_words, gate_scales, ou
             for part in leftovers:
                 finish_blend(chunk - 2, part)
             quantise_w(chunk, 1)
-            if 0 < chunk < LAST:
-                multiply_gate(chunk + 1)
             if chunk == LAST:
                 for sums, row_tile in EARLY_SUMS:
                     open_last(sums, row_tile)
@@ -381,6 +385,9 @@ def tile_nalu_kernel(tc, input_tensor, W_hat, M_hat, gate_words, gate_scales, ou
             quantise_w(chunk, 2)
             if 0 < chunk < LAST:
                 apply_gate(before, 0)
+            if chunk < LAST:
+                start_multiply_w(chunk)
+                multiply_gate(chunk + 1)
             if chunk == LAST:
                 for sums, row_tile in LATE_SUMS:
                     open_last(sums, row_tile)

@@ -35,6 +35,7 @@ SLABS = OUT // SLAB
 X_UNITS = [(0, range(0, 1)), (0, range(1, 2)), (0, range(2, 4))] + [
     (row_tile, range(2 * half, 2 * half + 2)) for row_tile in range(1, ROW_TILES) for half in range(2)
 ]
+HEAD_UNITS = X_UNITS[:3]
 EARLY_BANKS = "x_t_then_gate_sums"
 LATE_BANKS = ["log_sums", "add_sums"]
 EARLY_SUMS = [("log_sums", 2), ("log_sums", 3), ("add_sums", 2), ("log_sums", 0), ("add_sums", 0)]
@@ -66,9 +67,9 @@ def tile_nalu_kernel(tc, input_tensor, W_hat, M_hat, gate_words, gate_scales, ou
 
         x_rows = {}
 
-        def unit_tile(unit, name):
+        def unit_tile(unit, name, units=X_UNITS):
             size = len(unit[1])
-            count = sum(len(passes) == size for tile_of_rows, passes in X_UNITS)
+            count = sum(len(passes) == size for tile_of_rows, passes in units)
             return x_pool.tile([P, size * K_PASS], BF16, name=name, tag="%s_%d" % (name, size), bufs=count, align_bytes=64)
 
         def load_x(unit):
@@ -127,7 +128,7 @@ def tile_nalu_kernel(tc, input_tensor, W_hat, M_hat, gate_words, gate_scales, ou
 
         def clear_signs(unit):
             size = len(unit[1])
-            x_abs[unit] = stream.tile([P, size, 2, P], I32, name="x_abs")
+            x_abs[unit] = stream.tile([P, size, 2, P], I32, name="x_abs", bufs=4)
             nc.vector.tensor_scalar(
                 out=x_abs[unit][:],
                 in0=x_rows[unit][:].bitcast(I32).rearrange("r (g p w) -> r g w p", g=size, w=2),
@@ -135,6 +136,17 @@ def tile_nalu_kernel(tc, input_tensor, W_hat, M_hat, gate_words, gate_scales, ou
                 scalar2=None,
                 op0=ALU.bitwise_and,
             )
+
+        log_rows = {}
+
+        def take_log_of_rows(unit):
+            x_abs[unit] = stream.tile([P, len(unit[1]) * K_PASS], BF16, name="x_abs", bufs=4)
+            nc.vector.tensor_scalar(
+                out=x_abs[unit][:].bitcast(I32), in0=x_rows[unit][:].bitcast(I32),
+                scalar1=ABS_MASK, scalar2=None, op0=ALU.bitwise_and,
+            )
+            log_rows[unit] = unit_tile(unit, "log_rows", HEAD_UNITS)
+            nc.scalar.activation(out=log_rows[unit][:], in_=x_abs[unit][:], func=ACT.Ln, bias=EPS, scale=1.0)
 
         def transpose_abs(unit):
             size = len(unit[1])
@@ -151,9 +163,9 @@ def tile_nalu_kernel(tc, input_tensor, W_hat, M_hat, gate_words, gate_scales, ou
                 func=ACT.Ln, bias=EPS, scale=1.0,
             )
 
-        def transpose_x(unit):
+        def transpose_rows(unit, rows):
             size = len(unit[1])
-            words = x_rows[unit][:].bitcast(F32)
+            words = rows[unit][:].bitcast(F32)
             x_t[unit] = psum.tile([P, size, 2, P], F32, name="x_t", tag=EARLY_BANKS, bufs=4)
             for g in range(size):
                 for w in range(2):
@@ -161,11 +173,11 @@ def tile_nalu_kernel(tc, input_tensor, W_hat, M_hat, gate_words, gate_scales, ou
                         x_t[unit][:, g, w, :], words[:, 256 * g + w : 256 * (g + 1) : 2], identity[:]
                     )
 
-        def group_x(unit):
+        def group_rows(unit, grouped, name):
             size = len(unit[1])
-            x_grouped[unit] = unit_tile(unit, "x_grouped")
+            grouped[unit] = unit_tile(unit, name)
             nc.vector.tensor_copy(
-                out=x_grouped[unit][:].bitcast(F32).rearrange("p (g r w) -> p g r w", g=size, w=2),
+                out=grouped[unit][:].bitcast(F32).rearrange("p (g r w) -> p g r w", g=size, w=2),
                 in_=x_t[unit][:].rearrange("p g w r -> p g r w"),
             )
 
@@ -176,6 +188,12 @@ def tile_nalu_kernel(tc, input_tensor, W_hat, M_hat, gate_words, gate_scales, ou
                 scales=scales[:, row_tile, passes, :].rearrange("p g r -> p (g r)"),
                 in_=grouped[unit][:],
             )
+
+        def quantise_log(chunk, third):
+            lot = len(X_UNITS) // 3
+            if chunk == 0:
+                for unit in X_UNITS[lot * third : lot * (third + 1)]:
+                    quantise_unit(log_grouped, log_codes, log_scales, unit)
 
         w_codes = {}
         w_scales = {}
@@ -344,16 +362,37 @@ def tile_nalu_kernel(tc, input_tensor, W_hat, M_hat, gate_words, gate_scales, ou
         load_slab(1)
         load_gate_slab(1)
 
-        steps = [(clear_signs, -1), (transpose_abs, 0), (take_log, 0), (transpose_x, 2), (group_x, 3)]
-        clear_signs(X_UNITS[0])
-        for i in range(len(X_UNITS) + 3):
-            for step, behind in steps:
-                if 0 <= i - behind < len(X_UNITS):
-                    step(X_UNITS[i - behind])
+        for unit in HEAD_UNITS:
+            take_log_of_rows(unit)
+        late = X_UNITS[len(HEAD_UNITS) :]
+        for i in range(2):
+            transpose_rows(X_UNITS[i], x_rows)
+            clear_signs(late[i])
+            group_rows(X_UNITS[i], x_grouped, "x_grouped")
+        turned = []
+        for i, unit in enumerate(late):
+            transpose_abs(unit)
+            take_log(unit)
+            if i + 2 < len(late):
+                clear_signs(late[i + 2])
+            if i % 2 == 0 and i > 0:
+                group_rows(turned[-1], x_grouped, "x_grouped")
+            if i % 2 == 1:
+                turned.append(late[i // 2])
+                transpose_rows(turned[-1], x_rows)
+            if i == 0:
+                transpose_rows(X_UNITS[2], x_rows)
+                group_rows(X_UNITS[2], x_grouped, "x_grouped")
+        group_rows(turned[-1], x_grouped, "x_grouped")
+        for unit in late[len(turned) :]:
+            transpose_rows(unit, x_rows)
+            group_rows(unit, x_grouped, "x_grouped")
+        for unit in HEAD_UNITS:
+            transpose_rows(unit, log_rows)
+        for unit in HEAD_UNITS:
+            group_rows(unit, log_grouped, "log_grouped")
         for unit in X_UNITS:
             quantise_unit(x_grouped, x_codes, x_scales, unit)
-        for unit in X_UNITS:
-            quantise_unit(log_grouped, log_codes, log_scales, unit)
         multiply_gate(0)
 
         for chunk in range(CHUNKS):
@@ -367,12 +406,14 @@ def tile_nalu_kernel(tc, input_tensor, W_hat, M_hat, gate_words, gate_scales, ou
                 apply_gate(chunk - 2, part)
             quantise_w(chunk, 0)
 
+            quantise_log(chunk, 0)
             make_twice_w(chunk, 1)
             for part in parts[1:]:
                 squash_gate(before, part)
             for part in leftovers:
                 finish_blend(chunk - 2, part)
             quantise_w(chunk, 1)
+            quantise_log(chunk, 1)
             if chunk == LAST:
                 for sums, row_tile in EARLY_SUMS:
                     open_last(sums, row_tile)
@@ -383,6 +424,7 @@ def tile_nalu_kernel(tc, input_tensor, W_hat, M_hat, gate_words, gate_scales, ou
                 exponentiate(before, part)
                 start_blend(before, part)
             quantise_w(chunk, 2)
+            quantise_log(chunk, 2)
             if 0 < chunk < LAST:
                 apply_gate(before, 0)
             if chunk < LAST:
@@ -418,9 +460,10 @@ def tile_nalu_kernel(tc, input_tensor, W_hat, M_hat, gate_words, gate_scales, ou
         one_minus_g = blend.tile([P, ROW_TILES, width], F32, name="one_minus_g", bufs=1)
         nc.scalar.activation(out=one_minus_g[:], in_=gate_tanh[LAST, 0][:], func=ACT.Identity, scale=-0.5, bias=0.5)
         open_last("add_sums", ROW_TILES - 1)
+        multiply_last("add_sums", ROW_TILES - 1, range(3))
         for row_tile in range(ROW_TILES):
             multiply_last("log_sums", row_tile, range(3, 4))
-            multiply_last("add_sums", row_tile, range(0 if row_tile == ROW_TILES - 1 else 3, 4))
+            multiply_last("add_sums", row_tile, range(3, 4))
         apply_gate(LAST - 1, 1)
         for pair in range(PAIRS):
             finish_blend(LAST - 1, pair)

from contextlib import ExitStack

import concourse.mybir as mybir
from concourse.masks import make_identity

BF16 = mybir.dt.bfloat16
F32 = mybir.dt.float32
I32 = mybir.dt.int32
U32 = mybir.dt.uint32
U8 = mybir.dt.uint8
FP8X4 = mybir.dt.float8_e4m3fn_x4
ACT = mybir.ActivationFunctionType
ALU = mybir.AluOpType

B, IN, OUT = 512, 2048, 1536
EPS = 1e-07
FLOPS = 3 * 2 * B * IN * OUT

P = 128
PACK = 4
K_PASS = P * PACK
PASSES = IN // K_PASS
ROW_TILES = B // P
PAIRS = ROW_TILES // 2
BANK = 512
CHUNK = 256
CHUNK_WIDTHS = [CHUNK] * (OUT // CHUNK - 1) + [CHUNK // 2] * 2
CHUNK_STARTS = [sum(CHUNK_WIDTHS[:c]) for c in range(len(CHUNK_WIDTHS))]
CHUNKS = len(CHUNK_WIDTHS)
LAST = CHUNKS - 1
SHARE = [BANK // width for width in CHUNK_WIDTHS]
PARTS = [range(ROW_TILES // share) for share in SHARE]
SLAB = 2 * CHUNK
SLABS = OUT // SLAB
X_UNITS = [(0, range(0, 1)), (0, range(1, 2)), (0, range(2, 4))] + [
    (row_tile, range(2 * half, 2 * half + 2)) for row_tile in range(1, ROW_TILES) for half in range(2)
]
HEAD_UNITS = X_UNITS[:3]
EARLY_BANKS = "x_t_then_gate_sums"
LATE_BANKS = ["log_sums", "add_sums"]
EARLY_SUMS = [("log_sums", 2), ("log_sums", 3), ("add_sums", 2), ("log_sums", 0), ("add_sums", 0)]
LATE_SUMS = [("log_sums", 1), ("add_sums", 1)]
ABS_MASK = 0x7FFF7FFF


def tile_nalu_kernel(tc, input_tensor, W_hat, M_hat, gate_words, gate_scales, out):
    nc = tc.nc
    with ExitStack() as stack:
        keep = stack.enter_context(tc.tile_pool(name="keep", bufs=1))
        x_pool = stack.enter_context(tc.tile_pool(name="x_pool", bufs=1))
        slabs = stack.enter_context(tc.tile_pool(name="slabs", bufs=2))
        stream = stack.enter_context(tc.tile_pool(name="stream", bufs=3))
        blend = stack.enter_context(tc.tile_pool(name="blend", bufs=2))
        psum = stack.enter_context(tc.psum_pool(name="psum", bufs=2))
        stack.enter_context(tc.manual_schedule())

        identity = keep.tile([P, P], F32, name="identity")
        make_identity(nc, identity[:])

        x_codes = keep.tile([P, ROW_TILES, PASSES, P], U32, name="x_codes", align_bytes=64)
        x_scales = keep.tile([P, ROW_TILES, PASSES, P], U8, name="x_scales", align_bytes=64)
        log_codes = keep.tile([P, ROW_TILES, PASSES, P], U32, name="log_codes", align_bytes=64)
        log_scales = keep.tile([P, ROW_TILES, PASSES, P], U8, name="log_scales", align_bytes=64)

        gate_planes = keep.tile([P, OUT], U8, name="gate_planes", align_bytes=64)
        nc.vector.memset(gate_planes[:].bitcast(I32), 0)

        x_rows = {}

        def unit_tile(unit, name, units=X_UNITS):
            size = len(unit[1])
            count = sum(len(passes) == size for tile_of_rows, passes in units)
            return x_pool.tile([P, size * K_PASS], BF16, name=name, tag="%s_%d" % (name, size), bufs=count, align_bytes=64)

        def load_x(unit):
            row_tile, passes = unit
            x_rows[unit] = unit_tile(unit, "x_rows")
            nc.sync.dma_start(
                out=x_rows[unit][:],
                in_=input_tensor[P * row_tile : P * (row_tile + 1), K_PASS * passes.start : K_PASS * passes.stop],
            )

        def load_gate_planes():
            for quadrant in range(4):
                nc.sync.dma_start(
                    out=gate_planes[32 * quadrant : 32 * quadrant + 16, :].bitcast(I32),
                    in_=gate_scales[:, 4 * quadrant : 4 * quadrant + 4, :].bitcast(I32),
                )

        hat_slabs = {}

        def load_slab(slab):
            cols = slice(SLAB * slab, SLAB * (slab + 1))
            w_slab = slabs.tile([P, PASSES, PACK, SLAB], BF16, name="w_slab")
            m_slab = slabs.tile([P, PASSES, PACK, SLAB], BF16, name="m_slab")
            for g in range(PASSES):
                k_rows = slice(K_PASS * g, K_PASS * (g + 1))
                nc.sync.dma_start(
                    out=w_slab[:, g], in_=W_hat[k_rows, cols].rearrange("(p j) n -> p j n", j=PACK)
                )
                nc.sync.dma_start(
                    out=m_slab[:, g], in_=M_hat[k_rows, cols].rearrange("(p j) n -> p j n", j=PACK)
                )
            hat_slabs[slab] = (w_slab, m_slab)

        gate_slabs = {}

        def load_gate_slab(slab):
            cols = slice(SLAB * slab, SLAB * (slab + 1))
            gate_slabs[slab] = slabs.tile([P, PASSES, SLAB], I32, name="gate_slab", align_bytes=64)
            nc.sync.dma_start(
                out=gate_slabs[slab][:],
                in_=gate_words[:, :, cols, :].rearrange("g p n t -> p g (n t)").bitcast(I32),
            )

        def columns_in_slab(chunk):
            first = CHUNK_STARTS[chunk] % SLAB
            return CHUNK_STARTS[chunk] // SLAB, slice(first, first + CHUNK_WIDTHS[chunk])

        def columns(chunk):
            return slice(CHUNK_STARTS[chunk], CHUNK_STARTS[chunk] + CHUNK_WIDTHS[chunk])

        x_abs = {}
        abs_t = {}
        x_t = {}
        x_grouped = {}
        log_grouped = {}

        def clear_signs(unit):
            size = len(unit[1])
            x_abs[unit] = stream.tile([P, size, 2, P], I32, name="x_abs", bufs=4)
            nc.vector.tensor_scalar(
                out=x_abs[unit][:],
                in0=x_rows[unit][:].bitcast(I32).rearrange("r (g p w) -> r g w p", g=size, w=2),
                scalar1=ABS_MASK,
                scalar2=None,
                op0=ALU.bitwise_and,
            )

        log_rows = {}

        def take_log_of_rows(unit):
            x_abs[unit] = stream.tile([P, len(unit[1]) * K_PASS], BF16, name="x_abs", bufs=4)
            nc.vector.tensor_scalar(
                out=x_abs[unit][:].bitcast(I32), in0=x_rows[unit][:].bitcast(I32),
                scalar1=ABS_MASK, scalar2=None, op0=ALU.bitwise_and,
            )
            log_rows[unit] = unit_tile(unit, "log_rows", HEAD_UNITS)
            nc.scalar.activation(out=log_rows[unit][:], in_=x_abs[unit][:], func=ACT.Ln, bias=EPS, scale=1.0)

        def transpose_abs(unit):
            size = len(unit[1])
            abs_t[unit] = psum.tile([P, 2, size, P], F32, name="abs_t", tag=LATE_BANKS[X_UNITS.index(unit) % 2])
            for g in range(size):
                for w in range(2):
                    nc.tensor.transpose(abs_t[unit][:, w, g, :], x_abs[unit][:, g, w, :].bitcast(F32), identity[:])

        def take_log(unit):
            log_grouped[unit] = unit_tile(unit, "log_grouped")
            nc.scalar.activation(
                out=log_grouped[unit][:].rearrange("p (q w e) -> p q w e", w=2, e=2),
                in_=abs_t[unit][:].bitcast(BF16).rearrange("p w g (r e) -> p (g r) w e", e=2),
                func=ACT.Ln, bias=EPS, scale=1.0,
            )

        def transpose_rows(unit, rows):
            size = len(unit[1])
            words = rows[unit][:].bitcast(F32)
            x_t[unit] = psum.tile([P, size, 2, P], F32, name="x_t", tag=EARLY_BANKS, bufs=4)
            for g in range(size):
                for w in range(2):
                    nc.tensor.transpose(
                        x_t[unit][:, g, w, :], words[:, 256 * g + w : 256 * (g + 1) : 2], identity[:]
                    )

        def group_rows(unit, grouped, name):
            size = len(unit[1])
            grouped[unit] = unit_tile(unit, name)
            nc.vector.tensor_copy(
                out=grouped[unit][:].bitcast(F32).rearrange("p (g r w) -> p g r w", g=size, w=2),
                in_=x_t[unit][:].rearrange("p g w r -> p g r w"),
            )

        def quantise_unit(grouped, codes, scales, unit):
            row_tile, passes = unit[0], slice(unit[1].start, unit[1].stop)
            nc.vector.quantize_mx(
                out=codes[:, row_tile, passes, :].rearrange("p g r -> p (g r)").bitcast(FP8X4),
                scales=scales[:, row_tile, passes, :].rearrange("p g r -> p (g r)"),
                in_=grouped[unit][:],
            )

        def quantise_log(chunk, third):
            lot = len(X_UNITS) // 3
            if chunk == 0:
                for unit in X_UNITS[lot * third : lot * (third + 1)]:
                    quantise_unit(log_grouped, log_codes, log_scales, unit)

        w_codes = {}
        w_scales = {}
        w_grouped = {}

        def make_twice_w(chunk, g):
            slab, cols = columns_in_slab(chunk)
            w_slab, m_slab = hat_slabs[slab]
            width = CHUNK_WIDTHS[chunk]
            tanh_w = stream.tile([P, 2, width, 2], F32, name="tanh_w")
            tanh_m = stream.tile([P, 2, width, 2], F32, name="tanh_m")
            nc.scalar.activation(
                out=tanh_w[:],
                in_=w_slab[:, g, :, cols].rearrange("p (a b) n -> p b n a", b=2),
                func=ACT.Tanh,
            )
            nc.scalar.activation(
                out=tanh_m[:],
                in_=m_slab[:, g, :, cols].rearrange("p (a b) n -> p b n a", b=2),
                func=ACT.Tanh,
                scale=0.5,
            )
            w_grouped[g] = stream.tile([P, width, PACK], BF16, name="w_grouped", align_bytes=64)
            nc.vector.scalar_tensor_tensor(
                out=w_grouped[g][:].rearrange("p n (a b) -> p (n a) b", b=2),
                in0=tanh_m[:].rearrange("p b n a -> p (n a) b"),
                scalar=1.0,
                in1=tanh_w[:].rearrange("p b n a -> p (n a) b"),
                op0=ALU.add,
                op1=ALU.mult,
            )

        def quantise_w(chunk, g):
            if g == 0:
                width = CHUNK_WIDTHS[chunk]
                w_codes[chunk] = blend.tile([P, PASSES, width], U32, name="w_codes", align_bytes=64)
                w_scales[chunk] = blend.tile([P, PASSES, width], U8, name="w_scales", align_bytes=64)
            nc.vector.quantize_mx(
                out=w_codes[chunk][:, g, :].bitcast(FP8X4),
                scales=w_scales[chunk][:, g, :],
                in_=w_grouped[g][:].rearrange("p n j -> p (n j)"),
            )

        def multiply(bank, row_tile, lhs_codes, lhs_scales, rhs_of_pass, rhs_scale_of_pass, passes):
            for g in passes:
                nc.tensor.matmul_mx(
                    out=bank,
                    lhsT=lhs_codes[:, row_tile, g, :].bitcast(FP8X4),
                    lhsT_scale=lhs_scales[:, row_tile, g, :],
                    rhs=rhs_of_pass(g).bitcast(FP8X4),
                    rhs_scale=rhs_scale_of_pass(g),
                    start=(g == 0),
                    stop=(g == PASSES - 1),
                )

        gate_sums = {}
        log_sums = {}
        add_sums = {}
        gate_tanh = {}

        def multiply_gate(chunk):
            slab, cols = columns_in_slab(chunk)
            for part in PARTS[chunk]:
                gate_sums[chunk, part] = psum.tile(
                    [P, SHARE[chunk], CHUNK_WIDTHS[chunk]], F32, name="gate_sums", tag=EARLY_BANKS, bufs=4
                )
                for i in range(SHARE[chunk]):
                    multiply(
                        gate_sums[chunk, part][:, i, :], SHARE[chunk] * part + i, x_codes, x_scales,
                        lambda g: gate_slabs[slab][:, g, cols],
                        lambda g: gate_planes[4 * g : P, columns(chunk)],
                        range(PASSES),
                    )

        def multiply_by_w(bank, row_tile, lhs_codes, lhs_scales, chunk, passes):
            multiply(
                bank, row_tile, lhs_codes, lhs_scales,
                lambda g: w_codes[chunk][:, g, :],
                lambda g: w_scales[chunk][:, g, :],
                passes,
            )

        def start_multiply_w(chunk):
            log_sums[chunk, 0] = psum.tile([P, SHARE[chunk], CHUNK_WIDTHS[chunk]], F32, name="log_sums")
            multiply_by_w(log_sums[chunk, 0][:, 0, :], 0, log_codes, log_scales, chunk, range(PASSES - 1))

        def multiply_w(chunk):
            shape = [P, SHARE[chunk], CHUNK_WIDTHS[chunk]]
            for part in PARTS[chunk]:
                first = SHARE[chunk] * part
                if part > 0:
                    log_sums[chunk, part] = psum.tile(shape, F32, name="log_sums")
                for i in range(SHARE[chunk]):
                    done = PASSES - 1 if first + i == 0 else 0
                    multiply_by_w(
                        log_sums[chunk, part][:, i, :], first + i, log_codes, log_scales, chunk, range(done, PASSES)
                    )
                add_sums[chunk, part] = psum.tile(shape, F32, name="add_sums")
                for i in range(SHARE[chunk]):
                    multiply_by_w(add_sums[chunk, part][:, i, :], first + i, x_codes, x_scales, chunk, range(PASSES))

        last_sums = {}

        def open_last(sums, row_tile):
            tag, bufs = (EARLY_BANKS, 4) if row_tile >= 2 else (sums, 2)
            last_sums[sums, row_tile] = psum.tile([P, CHUNK_WIDTHS[LAST]], F32, name="last_sums", tag=tag, bufs=bufs)

        def multiply_last(sums, row_tile, passes):
            codes, scales = (log_codes, log_scales) if sums == "log_sums" else (x_codes, x_scales)
            multiply_by_w(last_sums[sums, row_tile][:], row_tile, codes, scales, LAST, passes)

        mult_path = {}
        diff = {}
        gated = {}

        def squash_gate(chunk, part):
            gate_tanh[chunk, part] = stream.tile([P, SHARE[chunk], CHUNK_WIDTHS[chunk]], F32, name="gate_tanh", bufs=4)
            nc.scalar.activation(
                out=gate_tanh[chunk, part][:], in_=gate_sums[chunk, part][:], func=ACT.Tanh, scale=0.5
            )

        def exponentiate(chunk, part):
            mult_path[chunk, part] = blend.tile([P, SHARE[chunk], CHUNK_WIDTHS[chunk]], F32, name="mult_path", bufs=3)
            nc.scalar.activation(out=mult_path[chunk, part][:], in_=log_sums[chunk, part][:], func=ACT.Exp, scale=0.5)

        def start_blend(chunk, part):
            shape = [P, SHARE[chunk], CHUNK_WIDTHS[chunk]]
            diff[chunk, part] = blend.tile(shape, F32, name="diff")
            nc.vector.scalar_tensor_tensor(
                out=diff[chunk, part][:], in0=add_sums[chunk, part][:], scalar=0.5, in1=mult_path[chunk, part][:],
                op0=ALU.mult, op1=ALU.subtract,
            )

        def rows_of_pair(chunk, pair):
            part, first = divmod(2 * pair, SHARE[chunk])
            return part, slice(first, first + 2)

        def apply_gate(chunk, pair):
            part, rows = rows_of_pair(chunk, pair)
            gated[chunk, pair] = blend.tile([P, 2, CHUNK_WIDTHS[chunk]], F32, name="gated")
            nc.vector.scalar_tensor_tensor(
                out=gated[chunk, pair][:], in0=gate_tanh[chunk, part][:, rows, :], scalar=1.0,
                in1=diff[chunk, part][:, rows, :], op0=ALU.add, op1=ALU.mult,
            )

        def store(chunk, pair, result):
            nc.sync.dma_start(
                out=out[2 * P * pair : 2 * P * (pair + 1), columns(chunk)].rearrange("(i p) n -> p i n", p=P),
                in_=result[:],
            )

        def finish_blend(chunk, pair):
            part, rows = rows_of_pair(chunk, pair)
            result = blend.tile([P, 2, CHUNK_WIDTHS[chunk]], F32, name="result", bufs=4)
            nc.vector.scalar_tensor_tensor(
                out=result[:], in0=gated[chunk, pair][:], scalar=0.5, in1=mult_path[chunk, part][:, rows, :],
                op0=ALU.mult, op1=ALU.add,
            )
            store(chunk, pair, result)

        for unit in X_UNITS:
            load_x(unit)
        load_slab(0)
        load_gate_planes()
        load_gate_slab(0)
        load_slab(1)
        load_gate_slab(1)

        for unit in HEAD_UNITS:
            take_log_of_rows(unit)
        late = X_UNITS[len(HEAD_UNITS) :]
        for i in range(2):
            transpose_rows(X_UNITS[i], x_rows)
            clear_signs(late[i])
            group_rows(X_UNITS[i], x_grouped, "x_grouped")
        turned = []
        for i, unit in enumerate(late):
            transpose_abs(unit)
            take_log(unit)
            if i + 2 < len(late):
                clear_signs(late[i + 2])
            if i % 2 == 0 and i > 0:
                group_rows(turned[-1], x_grouped, "x_grouped")
            if i % 2 == 1:
                turned.append(late[i // 2])
                transpose_rows(turned[-1], x_rows)
            if i == 0:
                transpose_rows(X_UNITS[2], x_rows)
                group_rows(X_UNITS[2], x_grouped, "x_grouped")
        group_rows(turned[-1], x_grouped, "x_grouped")
        for unit in late[len(turned) :]:
            transpose_rows(unit, x_rows)
            group_rows(unit, x_grouped, "x_grouped")
        for unit in HEAD_UNITS:
            transpose_rows(unit, log_rows)
        for unit in HEAD_UNITS:
            group_rows(unit, log_grouped, "log_grouped")
        for unit in X_UNITS:
            quantise_unit(x_grouped, x_codes, x_scales, unit)
        multiply_gate(0)

        for chunk in range(CHUNKS):
            before = chunk - 1
            parts = PARTS[before] if chunk > 0 else range(0)
            leftovers = PARTS[chunk - 2][1:] if chunk > 1 else range(0)
            make_twice_w(chunk, 0)
            for part in parts[:1]:
                squash_gate(before, part)
            for part in leftovers:
                apply_gate(chunk - 2, part)
            quantise_w(chunk, 0)

            quantise_log(chunk, 0)
            make_twice_w(chunk, 1)
            for part in parts[1:]:
                squash_gate(before, part)
            for part in leftovers:
                finish_blend(chunk - 2, part)
            quantise_w(chunk, 1)
            quantise_log(chunk, 1)
            if chunk == LAST:
                for sums, row_tile in EARLY_SUMS:
                    open_last(sums, row_tile)
                    multiply_last(sums, row_tile, range(2))

            make_twice_w(chunk, 2)
            for part in parts[:1]:
                exponentiate(before, part)
                start_blend(before, part)
            quantise_w(chunk, 2)
            quantise_log(chunk, 2)
            if 0 < chunk < LAST:
                apply_gate(before, 0)
            if chunk < LAST:
                start_multiply_w(chunk)
                multiply_gate(chunk + 1)
            if chunk == LAST:
                for sums, row_tile in LATE_SUMS:
                    open_last(sums, row_tile)
                    multiply_last(sums, row_tile, range(2))
                for sums, row_tile in EARLY_SUMS + LATE_SUMS:
                    multiply_last(sums, row_tile, range(2, 3))

            make_twice_w(chunk, 3)
            for part in parts[1:]:
                exponentiate(before, part)
            if chunk == LAST:
                apply_gate(before, 0)
            elif chunk > 0:
                finish_blend(before, 0)
            quantise_w(chunk, 3)
            for part in parts[1:]:
                start_blend(before, part)
            if chunk < LAST:
                multiply_w(chunk)
            chunk_end = CHUNK_STARTS[chunk] + CHUNK_WIDTHS[chunk]
            next_slab = chunk_end // SLAB + 1
            if chunk_end % SLAB == 0 and next_slab < SLABS:
                load_slab(next_slab)
                load_gate_slab(next_slab)

        width = CHUNK_WIDTHS[LAST]
        squash_gate(LAST, 0)
        one_minus_g = blend.tile([P, ROW_TILES, width], F32, name="one_minus_g", bufs=1)
        nc.scalar.activation(out=one_minus_g[:], in_=gate_tanh[LAST, 0][:], func=ACT.Identity, scale=-0.5, bias=0.5)
        open_last("add_sums", ROW_TILES - 1)
        multiply_last("add_sums", ROW_TILES - 1, range(3))
        for row_tile in range(ROW_TILES):
            multiply_last("log_sums", row_tile, range(3, 4))
            multiply_last("add_sums", row_tile, range(3, 4))
        apply_gate(LAST - 1, 1)
        for pair in range(PAIRS):
            finish_blend(LAST - 1, pair)
        last_m = blend.tile([P, ROW_TILES, width], F32, name="mult_path", bufs=3)
        gated_a = blend.tile([P, ROW_TILES, width], F32, name="gated")
        gated_m = blend.tile([P, ROW_TILES, width], F32, name="diff")
        for row_tile in range(ROW_TILES):
            nc.scalar.activation(out=last_m[:, row_tile, :], in_=last_sums["log_sums", row_tile][:], func=ACT.Exp, scale=0.5)
            nc.vector.scalar_tensor_tensor(
                out=gated_a[:, row_tile, :], in0=gate_tanh[LAST, 0][:, row_tile, :], scalar=1.0,
                in1=last_sums["add_sums", row_tile][:], op0=ALU.add, op1=ALU.mult,
            )
        for pair in range(PAIRS):
            rows = slice(2 * pair, 2 * pair + 2)
            nc.vector.tensor_tensor(
                out=gated_m[:, rows, :], in0=one_minus_g[:, rows, :], in1=last_m[:, rows, :], op=ALU.mult
            )
        for pair in range(PAIRS):
            rows = slice(2 * pair, 2 * pair + 2)
            result = blend.tile([P, 2, width], F32, name="result", bufs=4)
            nc.vector.scalar_tensor_tensor(
                out=result[:], in0=gated_a[:, rows, :], scalar=0.25, in1=gated_m[:, rows, :],
                op0=ALU.mult, op1=ALU.add,
            )
            store(LAST, pair, result)
